import numpy as np
import ml_dtypes


def mxq(x, axis, fmt="e4m3"):
    dtype, down = {"e4m3": (ml_dtypes.float8_e4m3fn, 7), "e5m2": (ml_dtypes.float8_e5m2, 14)}[fmt]
    v = np.moveaxis(np.asarray(x, np.float32).astype(ml_dtypes.bfloat16).astype(np.float64), axis, -1)
    blocks = v.reshape(v.shape[:-1] + (-1, 32))
    amax = np.abs(blocks).max(-1, keepdims=True)
    byte = np.maximum(np.where(amax > 0, np.frexp(amax)[1] - 1 + 127, 0) - down, 1)
    scale = np.exp2(byte - 127.0)
    codes = (blocks / scale).astype(np.float32).astype(dtype).astype(np.float64)
    return np.moveaxis((codes * scale).reshape(v.shape), -1, axis)


WIDE = False


def mx_kscale(k):
    if not WIDE:
        return np.ones(k)
    levels = np.array([10, -10, 5, -5, 0])
    if k % 512:
        return np.exp2(np.random.permutation(np.resize(levels, k // 32))).repeat(32)
    a = np.empty((k // 512, 16))
    for p in range(k // 512):
        a[p, :8] = np.random.permutation(np.resize(levels, 8))
        for g in range(8):
            far = levels[np.abs(levels - a[p, g]) >= 10]
            a[p, g + 8] = far[np.random.randint(len(far))]
    return np.exp2(a.ravel()).repeat(32)


BF16 = ml_dtypes.bfloat16


def bf(x):
    return np.asarray(x, np.float32).astype(BF16)


def f64(x):
    return np.asarray(x).astype(np.float64)


N, D, Q, CLIP, R = 4096, 1024, 128, 8, 16
MIX = 0.7
GAIN = 2.0


def unit(v):
    return v / np.sqrt((v * v).sum(-1, keepdims=True))


def setup_inputs():
    s = mx_kscale(D)
    base = np.random.standard_normal((N, D))
    return {"te": bf(unit(np.random.standard_normal((Q, D))) / s),
            "fe_n": bf(unit(base) * s),
            "loc_n": bf(unit(MIX * base + MIX * np.random.standard_normal((N, D))) * s),
            "glob_n": bf(unit(MIX * base + MIX * np.random.standard_normal((N, D))) * s),
            "logit_scale": bf(np.log(GAIN * np.sqrt(D)) + 0.1 * np.random.standard_normal(1)),
            "logit_bias": bf(-1.0 + 0.2 * np.random.standard_normal(1))}


def reference(te, fe_n, loc_n, glob_n, logit_scale, logit_bias):
    tq = mxq(f64(te), 1, "e4m3")
    ls = np.exp(f64(logit_scale))
    b = f64(logit_bias)
    ori = (tq @ mxq(f64(fe_n), 1, "e4m3").T) * ls + b
    loc = (tq @ mxq(f64(loc_n), 1, "e4m3").T) * ls + b
    glo = (tq @ mxq(f64(glob_n), 1, "e4m3").T) * ls + b
    fused = 0.9 * ori + 0.05 * loc + 0.05 * glo
    logits = fused.max(0, keepdims=True)
    x = logits.reshape(logits.shape[0], N // CLIP, CLIP)
    e = np.exp(x - x.max(-1, keepdims=True))
    w = e / e.sum(-1, keepdims=True)
    return (w * x).sum(-1)

@@ -1,0 +1,273 @@
+from contextlib import ExitStack
+
+import concourse.mybir as mybir
+from concourse.masks import make_identity
+
+F32 = mybir.dt.float32
+BF16 = mybir.dt.bfloat16
+U32 = mybir.dt.uint32
+U8 = mybir.dt.uint8
+FP8X4 = mybir.dt.float8_e4m3fn_x4
+ALU = mybir.AluOpType
+ACT = mybir.ActivationFunctionType
+AXIS = mybir.AxisListType
+
+P = 128
+FRAMES = 4096
+FEATURES = 1024
+QUERIES = 128
+CLIP = 8
+MAIN_WEIGHT = 0.9
+SIDE_WEIGHT = 0.05
+
+FLOPS = 2 * 3 * QUERIES * FRAMES * FEATURES
+
+TILES = FRAMES // P
+CLIPS_PER_PARTITION = TILES // CLIP
+K_PASS = 4 * P
+PASSES = FEATURES // K_PASS
+WORDS = FEATURES // 2
+WORD_BLOCKS = WORDS // P
+HALVES = WORD_BLOCKS // PASSES
+BLOCK_TILES = 4
+BLOCKS = TILES // BLOCK_TILES
+
+FE, LOC, GLOB = 0, 1, 2
+
+PSUM_BANKS = 8
+TRANSPOSE_BANKS = PSUM_BANKS - 2
+RUN = 4
+PAIR = 2
+VECTOR_EVERY = 6
+AHEAD = 3
+FOLD = 4
+OUT_ROWS = P // FOLD
+
+
+def work_list():
+    tiles = []
+    for block in range(BLOCKS):
+        for j in range(BLOCK_TILES):
+            tiles.append((LOC, block, j))
+            tiles.append((GLOB, block, j))
+        for j in range(BLOCK_TILES):
+            tiles.append((FE, block, j))
+    return tiles
+
+
+def tile_custommodel_pb_t_kernel(tc, te, fe_n, loc_n, glob_n, logit_scale, logit_bias, out):
+    nc = tc.nc
+    streams = {
+        FE: fe_n.rearrange("(p t) d -> p t d", t=TILES),
+        LOC: loc_n.rearrange("(p t) d -> p t d", t=TILES),
+        GLOB: glob_n.rearrange("(p t) d -> p t d", t=TILES),
+    }
+    tiles = work_list()
+    rounds = [tiles[i : i + RUN] for i in range(0, len(tiles), RUN)]
+
+    with ExitStack() as ctx:
+        keep = ctx.enter_context(tc.tile_pool(name="keep", bufs=1))
+        frames = ctx.enter_context(tc.tile_pool(name="frames", bufs=3 * AHEAD))
+        stage = ctx.enter_context(tc.tile_pool(name="stage", bufs=2 * RUN // PAIR))
+        packed = ctx.enter_context(tc.tile_pool(name="packed", bufs=3 * RUN // PAIR))
+        sums = ctx.enter_context(tc.tile_pool(name="sums", bufs=2))
+        banks = ctx.enter_context(tc.psum_pool(name="banks", bufs=TRANSPOSE_BANKS))
+        products = ctx.enter_context(tc.psum_pool(name="products", bufs=1))
+        ctx.enter_context(tc.manual_schedule())
+
+        loaded = {}
+
+        def load(stream, block, first, count):
+            if first == 0:
+                x = frames.tile([P, BLOCK_TILES, FEATURES], BF16, name="x")
+                loaded[(stream, block)] = x
+            t0 = block * BLOCK_TILES + first
+            nc.sync.dma_start(
+                out=loaded[(stream, block)][:, first : first + count, :],
+                in_=streams[stream][:, t0 : t0 + count, :],
+            )
+
+        def transpose_words(rows):
+            bank = banks.tile([P, WORD_BLOCKS, P], F32, name="bank")
+            words = rows.bitcast(F32)
+            for g in range(PASSES):
+                for u in range(HALVES):
+                    every_other = words[:, g * HALVES * P + u : (g + 1) * HALVES * P : HALVES]
+                    nc.tensor.transpose(bank[:, g * HALVES + u, :], every_other, identity[:])
+            return bank
+
+        def regroup(copy, bank, grouped_rows):
+            copy(
+                out=grouped_rows.bitcast(F32).rearrange("p (g r u) -> p g r u", g=PASSES, u=HALVES),
+                in_=bank[:].rearrange("p (g u) r -> p g r u", u=HALVES),
+            )
+
+        te_rows = keep.tile([P, FEATURES], BF16, name="te_rows")
+        nc.sync.dma_start(out=te_rows[:], in_=te)
+        scale_raw = keep.tile([P, 1], BF16, name="scale_raw")
+        nc.scalar.dma_start(out=scale_raw[:], in_=logit_scale.partition_broadcast(P))
+        bias_raw = keep.tile([P, 1], BF16, name="bias_raw")
+        nc.scalar.dma_start(out=bias_raw[:], in_=logit_bias.partition_broadcast(P))
+
+        for first in range(0, BLOCK_TILES, PAIR):
+            load(LOC, 0, first, PAIR)
+            load(GLOB, 0, first, PAIR)
+        load(FE, 0, 0, BLOCK_TILES)
+        for block in range(1, AHEAD):
+            for stream in (LOC, GLOB, FE):
+                load(stream, block, 0, BLOCK_TILES)
+
+        identity = keep.tile([P, P], F32, name="identity")
+        make_identity(nc, identity[:])
+
+        gain = keep.tile([P, 1], F32, name="gain")
+        nc.scalar.activation(out=gain[:], in_=scale_raw[:], func=ACT.Exp)
+
+        owner = keep.tile([P, OUT_ROWS], F32, name="owner")
+        nc.vector.tensor_reduce(
+            out=owner[:], in_=identity[:].rearrange("p (m b) -> p m b", b=FOLD), axis=AXIS.X, op=ALU.add
+        )
+        gather = keep.tile([P, FOLD, OUT_ROWS], F32, name="gather")
+        nc.vector.tensor_copy(out=gather[:], in_=owner[:].unsqueeze(1).to_broadcast([P, FOLD, OUT_ROWS]))
+        place = keep.tile([P, FOLD], F32, name="place")
+        nc.vector.tensor_reduce(
+            out=place[:], in_=identity[:].rearrange("p (m b) -> p b m", b=FOLD), axis=AXIS.X, op=ALU.add
+        )
+
+        te_bank = transpose_words(te_rows[:])
+        te_grouped = keep.tile([P, FEATURES], BF16, name="te_grouped", align_bytes=64)
+        regroup(nc.vector.tensor_copy, te_bank, te_grouped[:])
+        te_codes = keep.tile([P, PASSES * QUERIES], U32, name="te_codes", align_bytes=64)
+        te_scales = keep.tile([P, PASSES * QUERIES], U8, name="te_scales", align_bytes=64)
+        nc.vector.quantize_mx(out=te_codes[:].bitcast(FP8X4), scales=te_scales[:], in_=te_grouped[:])
+        bias = keep.tile([P, 1], F32, name="bias")
+        nc.vector.tensor_copy(out=bias[:], in_=bias_raw[:])
+        main_gain = keep.tile([P, 1], F32, name="main_gain")
+        nc.vector.tensor_scalar_mul(out=main_gain[:], in0=gain[:], scalar1=MAIN_WEIGHT)
+        side_gain = keep.tile([P, 1], F32, name="side_gain")
+        nc.vector.tensor_scalar_mul(out=side_gain[:], in0=gain[:], scalar1=SIDE_WEIGHT)
+
+        logits = keep.tile([P, CLIPS_PER_PARTITION, CLIP], F32, name="logits")
+
+        def transpose_round(step):
+            filled = []
+            for stream, block, j in rounds[step]:
+                filled.append(transpose_words(loaded[(stream, block)][:, j, :]))
+                if j == BLOCK_TILES - 1 and block + AHEAD < BLOCKS:
+                    load(stream, block + AHEAD, 0, BLOCK_TILES)
+            pairs = []
+            for n, bank in enumerate(filled):
+                if n % PAIR == 0:
+                    grouped = stage.tile([P, PAIR * FEATURES], BF16, name="grouped", align_bytes=64)
+                    pairs.append(grouped)
+                copy = nc.vector.tensor_copy if (step * RUN + n) % VECTOR_EVERY == 0 else nc.scalar.copy
+                s = n % PAIR
+                regroup(copy, bank, pairs[-1][:, s * FEATURES : (s + 1) * FEATURES])
+            return pairs
+
+        def quantise_round(pairs):
+            quantised = []
+            for grouped in pairs:
+                codes = packed.tile([P, PAIR * PASSES * P], U32, name="codes", align_bytes=64)
+                scales = packed.tile([P, PAIR * PASSES * P], U8, name="scales", align_bytes=64)
+                nc.vector.quantize_mx(out=codes[:].bitcast(FP8X4), scales=scales[:], in_=grouped[:])
+                quantised.append((codes, scales))
+            return quantised
+
+        current = {}
+
+        def multiply_round(step, quantised):
+            for n, (stream, block, j) in enumerate(rounds[step]):
+                codes, scales = quantised[n // PAIR]
+                if j == 0 and stream == FE:
+                    current["main"] = products.tile([P, BLOCK_TILES * QUERIES], F32, name="main")
+                if j == 0 and stream == LOC:
+                    current["side"] = products.tile([P, BLOCK_TILES * QUERIES], F32, name="side")
+                product = current["main"] if stream == FE else current["side"]
+                for g in range(PASSES):
+                    cols = slice(((n % PAIR) * PASSES + g) * P, ((n % PAIR) * PASSES + g + 1) * P)
+                    te_cols = slice(g * QUERIES, (g + 1) * QUERIES)
+                    nc.tensor.matmul_mx(
+                        out=product[:, j * QUERIES : (j + 1) * QUERIES],
+                        lhsT=codes[:, cols].bitcast(FP8X4),
+                        lhsT_scale=scales[:, cols],
+                        rhs=te_codes[:, te_cols].bitcast(FP8X4),
+                        rhs_scale=te_scales[:, te_cols],
+                        start=(stream != GLOB and g == 0),
+                        stop=(stream != LOC and g == PASSES - 1),
+                    )
+                if j == BLOCK_TILES - 1 and stream == GLOB:
+                    current["weighted"] = sums.tile([P, BLOCK_TILES * QUERIES], F32, name="weighted")
+                    nc.scalar.activation(
+                        out=current["weighted"][:],
+                        in_=product[:],
+                        func=ACT.Identity,
+                        scale=side_gain[:, 0:1],
+                        bias=bias[:, 0:1],
+                    )
+                if j == BLOCK_TILES - 1 and stream == FE:
+                    fused = sums.tile([P, BLOCK_TILES, QUERIES], F32, name="fused")
+                    nc.vector.scalar_tensor_tensor(
+                        out=fused[:].rearrange("p t q -> p (t q)"),
+                        in0=product[:],
+                        scalar=main_gain[:, 0:1],
+                        in1=current["weighted"][:],
+                        op0=ALU.mult,
+                        op1=ALU.add,
+                    )
+                    nc.vector.tensor_reduce(
+                        out=logits[:].rearrange("p c j -> p (c j)")[:, block * BLOCK_TILES : (block + 1) * BLOCK_TILES],
+                        in_=fused[:],
+                        axis=AXIS.X,
+                        op=ALU.max,
+                    )
+
+        grouped_of = {}
+        quantised_of = {}
+        for step in range(len(rounds) + 2):
+            if step < len(rounds):
+                grouped_of[step] = transpose_round(step)
+            if 1 <= step <= len(rounds):
+                quantised_of[step - 1] = quantise_round(grouped_of[step - 1])
+            if step >= 2:
+                multiply_round(step - 2, quantised_of[step - 2])
+
+        shape = [P, CLIPS_PER_PARTITION, CLIP]
+        top = keep.tile([P, CLIPS_PER_PARTITION], F32, name="top")
+        nc.vector.tensor_reduce(out=top[:], in_=logits[:], axis=AXIS.X, op=ALU.max)
+        shifted = keep.tile(shape, F32, name="shifted")
+        nc.vector.tensor_tensor(
+            out=shifted[:], in0=logits[:], in1=top[:].unsqueeze(2).to_broadcast(shape), op=ALU.subtract
+        )
+        terms = keep.tile([P, 2] + shape[1:], F32, name="terms")
+        nc.scalar.activation(out=terms[:, 0], in_=shifted[:], func=ACT.Exp)
+        nc.vector.tensor_tensor(out=terms[:, 1], in0=terms[:, 0], in1=logits[:], op=ALU.mult)
+        totals = keep.tile([P, 2 * CLIPS_PER_PARTITION], F32, name="totals")
+        nc.vector.tensor_reduce(
+            out=totals[:], in_=terms[:].rearrange("p h c j -> p (h c) j"), axis=AXIS.X, op=ALU.add
+        )
+
+        wide = [P, FOLD, 2 * CLIPS_PER_PARTITION]
+        spread = keep.tile(wide, F32, name="spread")
+        nc.vector.tensor_tensor(
+            out=spread[:],
+            in0=totals[:].unsqueeze(1).to_broadcast(wide),
+            in1=place[:].unsqueeze(2).to_broadcast(wide),
+            op=ALU.mult,
+        )
+        folded = banks.tile([P, FOLD, 2, CLIPS_PER_PARTITION], F32, name="folded", tag="bank")
+        nc.tensor.matmul(
+            out=folded[:].rearrange("p b h c -> p (b h c)"),
+            lhsT=gather[:].rearrange("p r m -> p (r m)"),
+            rhs=spread[:].rearrange("p b k -> p (b k)"),
+            start=True,
+            stop=True,
+        )
+        inverse = keep.tile([P, FOLD, CLIPS_PER_PARTITION], F32, name="inverse")
+        nc.vector.reciprocal(out=inverse[:], in_=folded[:, :, 0, :])
+        pooled = keep.tile([P, FOLD, CLIPS_PER_PARTITION], F32, name="pooled")
+        nc.vector.tensor_tensor(out=pooled[:], in0=folded[:, :, 1, :], in1=inverse[:], op=ALU.mult)
+        nc.sync.dma_start(
+            out=out.rearrange("o (m k) -> (o m) k", k=FOLD * CLIPS_PER_PARTITION),
+            in_=pooled[0:OUT_ROWS].rearrange("p b c -> p (b c)"),
+        )

@@ -29,47 +29,47 @@ PASSES = FEATURES // K_PASS
 WORDS = FEATURES // 2
 WORD_BLOCKS = WORDS // P
 HALVES = WORD_BLOCKS // PASSES
-BLOCK_TILES = 4
-BLOCKS = TILES // BLOCK_TILES
+MX_BLOCKS = P // 8
+HALF_BLOCK = 16
 
 FE, LOC, GLOB = 0, 1, 2
+ORDER = (FE, LOC, GLOB)
 
 PSUM_BANKS = 8
 TRANSPOSE_BANKS = PSUM_BANKS - 2
-RUN = 4
 PAIR = 2
-VECTOR_EVERY = 6
-AHEAD = 3
-FOLD = 4
-OUT_ROWS = P // FOLD
+AHEAD = 8
+ROUNDS = [PAIR] * 15 + [1, 1]
+GROUPS = [4] * 7 + [2, 1, 1]
+STEPPED_ROUNDS = 1
+LAG = 2
 
 
-def work_list():
-    tiles = []
-    for block in range(BLOCKS):
-        for j in range(BLOCK_TILES):
-            tiles.append((LOC, block, j))
-            tiles.append((GLOB, block, j))
-        for j in range(BLOCK_TILES):
-            tiles.append((FE, block, j))
-    return tiles
+def split(counts):
+    runs = []
+    first = 0
+    for count in counts:
+        runs.append(list(range(first, first + count)))
+        first += count
+    return runs
 
 
 def tile_custommodel_pb_t_kernel(tc, te, fe_n, loc_n, glob_n, logit_scale, logit_bias, out):
     nc = tc.nc
-    streams = {
-        FE: fe_n.rearrange("(p t) d -> p t d", t=TILES),
-        LOC: loc_n.rearrange("(p t) d -> p t d", t=TILES),
-        GLOB: glob_n.rearrange("(p t) d -> p t d", t=TILES),
-    }
-    tiles = work_list()
-    rounds = [tiles[i : i + RUN] for i in range(0, len(tiles), RUN)]
+    streams = {}
+    for stream, hbm in ((FE, fe_n), (LOC, loc_n), (GLOB, glob_n)):
+        streams[stream] = hbm.rearrange("(c p j) d -> p c j d", c=CLIPS_PER_PARTITION, j=CLIP)
+
+    rounds = split(ROUNDS)
+    groups = split(GROUPS)
+    group_of = {t: group for group in groups for t in group}
 
     with ExitStack() as ctx:
         keep = ctx.enter_context(tc.tile_pool(name="keep", bufs=1))
         frames = ctx.enter_context(tc.tile_pool(name="frames", bufs=3 * AHEAD))
-        stage = ctx.enter_context(tc.tile_pool(name="stage", bufs=2 * RUN // PAIR))
-        packed = ctx.enter_context(tc.tile_pool(name="packed", bufs=3 * RUN // PAIR))
+        ordered = ctx.enter_context(tc.tile_pool(name="ordered", bufs=4))
+        stage = ctx.enter_context(tc.tile_pool(name="stage", bufs=6))
+        packed = ctx.enter_context(tc.tile_pool(name="packed", bufs=15))
         sums = ctx.enter_context(tc.tile_pool(name="sums", bufs=2))
         banks = ctx.enter_context(tc.psum_pool(name="banks", bufs=TRANSPOSE_BANKS))
         products = ctx.enter_context(tc.psum_pool(name="products", bufs=1))
@@ -77,24 +77,31 @@ def tile_custommodel_pb_t_kernel(tc, te, fe_n, loc_n, glob_n, logit_scale, logit
 
         loaded = {}
 
-        def load(stream, block, first, count):
-            if first == 0:
-                x = frames.tile([P, BLOCK_TILES, FEATURES], BF16, name="x")
-                loaded[(stream, block)] = x
-            t0 = block * BLOCK_TILES + first
-            nc.sync.dma_start(
-                out=loaded[(stream, block)][:, first : first + count, :],
-                in_=streams[stream][:, t0 : t0 + count, :],
+        def load(stream, step, piece=PAIR):
+            first, count = rounds[step][0], len(rounds[step])
+            x = frames.tile([P, count, FEATURES], BF16, name="x")
+            loaded[(stream, step)] = x
+            c, j = first // CLIP, first % CLIP
+            for n in range(0, count, piece):
+                m = min(count, n + piece)
+                nc.sync.dma_start(out=x[:, n:m, :], in_=streams[stream][:, c, j + n : j + m, :])
+
+        def reorder(out, rows):
+            nc.vector.tensor_copy(
+                out=out.rearrange("p (k u s i) -> p k u s i", u=HALVES, s=MX_BLOCKS, i=HALF_BLOCK),
+                in_=rows.rearrange("p (k s u i) -> p k u s i", u=HALVES, s=MX_BLOCKS, i=HALF_BLOCK),
             )
 
-        def transpose_words(rows):
-            bank = banks.tile([P, WORD_BLOCKS, P], F32, name="bank")
+        def transpose_words(rows, ordered_words, bank):
             words = rows.bitcast(F32)
             for g in range(PASSES):
                 for u in range(HALVES):
-                    every_other = words[:, g * HALVES * P + u : (g + 1) * HALVES * P : HALVES]
-                    nc.tensor.transpose(bank[:, g * HALVES + u, :], every_other, identity[:])
-            return bank
+                    n = g * HALVES + u
+                    if ordered_words:
+                        half = words[:, n * P : (n + 1) * P]
+                    else:
+                        half = words[:, g * HALVES * P + u : (g + 1) * HALVES * P : HALVES]
+                    nc.tensor.transpose(bank[:, n, :], half, identity[:])
 
         def regroup(copy, bank, grouped_rows):
             copy(
@@ -103,134 +110,195 @@ def tile_custommodel_pb_t_kernel(tc, te, fe_n, loc_n, glob_n, logit_scale, logit
             )
 
         te_rows = keep.tile([P, FEATURES], BF16, name="te_rows")
-        nc.sync.dma_start(out=te_rows[:], in_=te)
         scale_raw = keep.tile([P, 1], BF16, name="scale_raw")
-        nc.scalar.dma_start(out=scale_raw[:], in_=logit_scale.partition_broadcast(P))
         bias_raw = keep.tile([P, 1], BF16, name="bias_raw")
+        load(ORDER[0], 0, 1)
+        nc.sync.dma_start(out=te_rows[:], in_=te)
+        for stream in ORDER[1:]:
+            load(stream, 0, 1)
+        nc.scalar.dma_start(out=scale_raw[:], in_=logit_scale.partition_broadcast(P))
         nc.scalar.dma_start(out=bias_raw[:], in_=logit_bias.partition_broadcast(P))
-
-        for first in range(0, BLOCK_TILES, PAIR):
-            load(LOC, 0, first, PAIR)
-            load(GLOB, 0, first, PAIR)
-        load(FE, 0, 0, BLOCK_TILES)
-        for block in range(1, AHEAD):
-            for stream in (LOC, GLOB, FE):
-                load(stream, block, 0, BLOCK_TILES)
+        for step in range(1, AHEAD):
+            for stream in ORDER:
+                load(stream, step)
 
         identity = keep.tile([P, P], F32, name="identity")
         make_identity(nc, identity[:])
+        pooled_parts = keep.tile([P, 2, P], F32, name="pooled_parts")
+        nc.gpsimd.memset(pooled_parts[:], 0.0)
 
+        blank = keep.tile([P, 1], F32, name="blank")
+        nc.gpsimd.memset(blank[:], 0.0)
+        one = keep.tile([P, 1], F32, name="one")
+        nc.scalar.activation(out=one[:], in_=blank[:], func=ACT.Exp)
         gain = keep.tile([P, 1], F32, name="gain")
-        nc.scalar.activation(out=gain[:], in_=scale_raw[:], func=ACT.Exp)
 
-        owner = keep.tile([P, OUT_ROWS], F32, name="owner")
-        nc.vector.tensor_reduce(
-            out=owner[:], in_=identity[:].rearrange("p (m b) -> p m b", b=FOLD), axis=AXIS.X, op=ALU.add
-        )
-        gather = keep.tile([P, FOLD, OUT_ROWS], F32, name="gather")
-        nc.vector.tensor_copy(out=gather[:], in_=owner[:].unsqueeze(1).to_broadcast([P, FOLD, OUT_ROWS]))
-        place = keep.tile([P, FOLD], F32, name="place")
-        nc.vector.tensor_reduce(
-            out=place[:], in_=identity[:].rearrange("p (m b) -> p b m", b=FOLD), axis=AXIS.X, op=ALU.add
-        )
+        te_codes = {}
+        te_scales = {}
 
-        te_bank = transpose_words(te_rows[:])
-        te_grouped = keep.tile([P, FEATURES], BF16, name="te_grouped", align_bytes=64)
-        regroup(nc.vector.tensor_copy, te_bank, te_grouped[:])
-        te_codes = keep.tile([P, PASSES * QUERIES], U32, name="te_codes", align_bytes=64)
-        te_scales = keep.tile([P, PASSES * QUERIES], U8, name="te_scales", align_bytes=64)
-        nc.vector.quantize_mx(out=te_codes[:].bitcast(FP8X4), scales=te_scales[:], in_=te_grouped[:])
+        def prepare_te():
+            te_ordered = keep.tile([P, FEATURES], BF16, name="te_ordered")
+            reorder(te_ordered[:], te_rows[:])
+            for ordered_words, rows in ((True, te_ordered), (False, te_rows)):
+                te_bank = products.tile([P, WORD_BLOCKS, P], F32, name="te_bank", tag="main" if ordered_words else "side")
+                transpose_words(rows[:], ordered_words, te_bank)
+                te_grouped = keep.tile([P, FEATURES], BF16, name="te_grouped%d" % ordered_words, align_bytes=64)
+                regroup(nc.vector.tensor_copy, te_bank, te_grouped[:])
+                codes = keep.tile([P, PASSES * QUERIES], U32, name="te_codes%d" % ordered_words, align_bytes=64)
+                scales = keep.tile([P, PASSES * QUERIES], U8, name="te_scales%d" % ordered_words, align_bytes=64)
+                nc.vector.quantize_mx(out=codes[:].bitcast(FP8X4), scales=scales[:], in_=te_grouped[:])
+                te_codes[ordered_words] = codes
+                te_scales[ordered_words] = scales
+
         bias = keep.tile([P, 1], F32, name="bias")
-        nc.vector.tensor_copy(out=bias[:], in_=bias_raw[:])
         main_gain = keep.tile([P, 1], F32, name="main_gain")
-        nc.vector.tensor_scalar_mul(out=main_gain[:], in0=gain[:], scalar1=MAIN_WEIGHT)
         side_gain = keep.tile([P, 1], F32, name="side_gain")
-        nc.vector.tensor_scalar_mul(out=side_gain[:], in0=gain[:], scalar1=SIDE_WEIGHT)
 
         logits = keep.tile([P, CLIPS_PER_PARTITION, CLIP], F32, name="logits")
 
-        def transpose_round(step):
-            filled = []
-            for stream, block, j in rounds[step]:
-                filled.append(transpose_words(loaded[(stream, block)][:, j, :]))
-                if j == BLOCK_TILES - 1 and block + AHEAD < BLOCKS:
-                    load(stream, block + AHEAD, 0, BLOCK_TILES)
-            pairs = []
-            for n, bank in enumerate(filled):
-                if n % PAIR == 0:
-                    grouped = stage.tile([P, PAIR * FEATURES], BF16, name="grouped", align_bytes=64)
-                    pairs.append(grouped)
-                copy = nc.vector.tensor_copy if (step * RUN + n) % VECTOR_EVERY == 0 else nc.scalar.copy
-                s = n % PAIR
-                regroup(copy, bank, pairs[-1][:, s * FEATURES : (s + 1) * FEATURES])
-            return pairs
+        def is_ordered(stream, step):
+            return stream != FE and step >= STEPPED_ROUNDS
 
-        def quantise_round(pairs):
-            quantised = []
-            for grouped in pairs:
-                codes = packed.tile([P, PAIR * PASSES * P], U32, name="codes", align_bytes=64)
-                scales = packed.tile([P, PAIR * PASSES * P], U8, name="scales", align_bytes=64)
-                nc.vector.quantize_mx(out=codes[:].bitcast(FP8X4), scales=scales[:], in_=grouped[:])
-                quantised.append((codes, scales))
-            return quantised
+        rows_of = {}
 
-        current = {}
+        def reorder_rows(stream, step):
+            x = loaded[(stream, step)]
+            count = len(rounds[step])
+            if is_ordered(stream, step):
+                r = ordered.tile([P, count, FEATURES], BF16, name="r")
+                reorder(r[:].rearrange("p t d -> p (t d)"), x[:].rearrange("p t d -> p (t d)"))
+                rows_of[(stream, step)] = r
+            else:
+                rows_of[(stream, step)] = x
 
-        def multiply_round(step, quantised):
-            for n, (stream, block, j) in enumerate(rounds[step]):
-                codes, scales = quantised[n // PAIR]
-                if j == 0 and stream == FE:
-                    current["main"] = products.tile([P, BLOCK_TILES * QUERIES], F32, name="main")
-                if j == 0 and stream == LOC:
-                    current["side"] = products.tile([P, BLOCK_TILES * QUERIES], F32, name="side")
-                product = current["main"] if stream == FE else current["side"]
-                for g in range(PASSES):
-                    cols = slice(((n % PAIR) * PASSES + g) * P, ((n % PAIR) * PASSES + g + 1) * P)
-                    te_cols = slice(g * QUERIES, (g + 1) * QUERIES)
-                    nc.tensor.matmul_mx(
-                        out=product[:, j * QUERIES : (j + 1) * QUERIES],
-                        lhsT=codes[:, cols].bitcast(FP8X4),
-                        lhsT_scale=scales[:, cols],
-                        rhs=te_codes[:, te_cols].bitcast(FP8X4),
-                        rhs_scale=te_scales[:, te_cols],
-                        start=(stream != GLOB and g == 0),
-                        stop=(stream != LOC and g == PASSES - 1),
-                    )
-                if j == BLOCK_TILES - 1 and stream == GLOB:
-                    current["weighted"] = sums.tile([P, BLOCK_TILES * QUERIES], F32, name="weighted")
-                    nc.scalar.activation(
-                        out=current["weighted"][:],
-                        in_=product[:],
-                        func=ACT.Identity,
-                        scale=side_gain[:, 0:1],
-                        bias=bias[:, 0:1],
-                    )
-                if j == BLOCK_TILES - 1 and stream == FE:
-                    fused = sums.tile([P, BLOCK_TILES, QUERIES], F32, name="fused")
-                    nc.vector.scalar_tensor_tensor(
-                        out=fused[:].rearrange("p t q -> p (t q)"),
-                        in0=product[:],
-                        scalar=main_gain[:, 0:1],
-                        in1=current["weighted"][:],
-                        op0=ALU.mult,
-                        op1=ALU.add,
-                    )
-                    nc.vector.tensor_reduce(
-                        out=logits[:].rearrange("p c j -> p (c j)")[:, block * BLOCK_TILES : (block + 1) * BLOCK_TILES],
-                        in_=fused[:],
-                        axis=AXIS.X,
-                        op=ALU.max,
-                    )
+        def transpose_rows(stream, step, vector_copies=()):
+            count = len(rounds[step])
+            grouped = stage.tile([P, count * FEATURES], BF16, name="grouped", align_bytes=64)
+            for n in range(count):
+                bank = banks.tile([P, WORD_BLOCKS, P], F32, name="bank")
+                transpose_words(rows_of[(stream, step)][:, n, :], is_ordered(stream, step), bank)
+                copy = nc.vector.tensor_copy if n in vector_copies else nc.scalar.copy
+                regroup(copy, bank, grouped[:, n * FEATURES : (n + 1) * FEATURES])
+            if step + AHEAD < len(rounds):
+                load(stream, step + AHEAD)
+            return grouped
+
+        quantised = {}
+
+        def quantise(stream, step, grouped):
+            count = len(rounds[step])
+            codes = packed.tile([P, count * PASSES * P], U32, name="codes", align_bytes=64)
+            scales = packed.tile([P, count * PASSES * P], U8, name="scales", align_bytes=64)
+            nc.vector.quantize_mx(out=codes[:].bitcast(FP8X4), scales=scales[:], in_=grouped[:])
+            for n, t in enumerate(rounds[step]):
+                quantised[(stream, t)] = (codes, scales, n, is_ordered(stream, step))
+
+        def multiply(group):
+            if len(group) == max(GROUPS):
+                side = products.tile([P, max(GROUPS) * QUERIES], F32, name="side")
+                main = products.tile([P, max(GROUPS) * QUERIES], F32, name="main")
+            else:
+                side = banks.tile([P, max(GROUPS) * QUERIES], F32, name="last_side", tag="bank")
+                main = banks.tile([P, max(GROUPS) * QUERIES], F32, name="last_main", tag="bank")
+            for j, t in enumerate(group):
+                for stream in (LOC, GLOB, FE):
+                    codes, scales, n, ordered_words = quantised[(stream, t)]
+                    product = main if stream == FE else side
+                    for g in range(PASSES):
+                        cols = slice((n * PASSES + g) * P, (n * PASSES + g + 1) * P)
+                        te_cols = slice(g * QUERIES, (g + 1) * QUERIES)
+                        nc.tensor.matmul_mx(
+                            out=product[:, j * QUERIES : (j + 1) * QUERIES],
+                            lhsT=codes[:, cols].bitcast(FP8X4),
+                            lhsT_scale=scales[:, cols],
+                            rhs=te_codes[ordered_words][:, te_cols].bitcast(FP8X4),
+                            rhs_scale=te_scales[ordered_words][:, te_cols],
+                            start=(stream != GLOB and g == 0),
+                            stop=(stream != LOC and g == PASSES - 1),
+                        )
+            return group, main, side
+
+        def weigh(done):
+            group, main, side = done
+            weighted = sums.tile([P, max(GROUPS) * QUERIES], F32, name="weighted")
+            width = len(group) * QUERIES
+            nc.scalar.activation(
+                out=weighted[:, :width],
+                in_=side[:, :width],
+                func=ACT.Identity,
+                scale=side_gain[:, 0:1],
+                bias=bias[:, 0:1],
+            )
+            return weighted
+
+        def fuse(done, weighted):
+            group, main, side = done
+            width = len(group) * QUERIES
+            fused = sums.tile([P, max(GROUPS) * QUERIES], F32, name="fused")
+            nc.vector.scalar_tensor_tensor(
+                out=fused[:, :width],
+                in0=main[:, :width],
+                scalar=main_gain[:, 0:1],
+                in1=weighted[:, :width],
+                op0=ALU.mult,
+                op1=ALU.add,
+            )
+            nc.vector.tensor_reduce(
+                out=logits[:].rearrange("p c j -> p (c j)")[:, group[0] : group[-1] + 1],
+                in_=fused[:, :width].rearrange("p (t q) -> p t q", q=QUERIES),
+                axis=AXIS.X,
+                op=ALU.max,
+            )
 
         grouped_of = {}
-        quantised_of = {}
-        for step in range(len(rounds) + 2):
+        finished = None
+        last_round_of = {}
+        for n, group in enumerate(groups):
+            last_round_of[n] = [i for i in range(len(rounds)) if group[-1] in rounds[i]][0]
+        for stream in ORDER:
+            reorder_rows(stream, 0)
+        next_group = 0
+        for step in range(len(rounds) + LAG):
+            weighted = None
             if step < len(rounds):
-                grouped_of[step] = transpose_round(step)
+                for stream in ORDER:
+                    grouped_of[(stream, step)] = transpose_rows(
+                        stream, step, (len(rounds[step]) - 1,) if step >= len(rounds) - 2 and stream == LOC else ()
+                    )
+                    if stream == ORDER[0] and finished:
+                        weighted = weigh(finished)
+                    if stream == ORDER[0] and step == 0:
+                        prepare_te()
+                if step == 1:
+                    nc.scalar.activation(out=gain[:], in_=scale_raw[:], func=ACT.Exp)
+            elif finished:
+                weighted = weigh(finished)
+            ops = []
             if 1 <= step <= len(rounds):
-                quantised_of[step - 1] = quantise_round(grouped_of[step - 1])
-            if step >= 2:
-                multiply_round(step - 2, quantised_of[step - 2])
+                ops += [("q", stream) for stream in ORDER]
+            if step + 1 < len(rounds):
+                ops = ops[:1] + [("r", FE), ("r", LOC), ("r", GLOB)] + ops[1:]
+            for kind, stream in ops:
+                if kind == "q":
+                    quantise(stream, step - 1, grouped_of[(stream, step - 1)])
+                else:
+                    reorder_rows(stream, step + 1)
+            if step == 2:
+                nc.vector.tensor_copy(out=bias[:], in_=bias_raw[:])
+                nc.vector.tensor_scalar_mul(out=main_gain[:], in0=gain[:], scalar1=MAIN_WEIGHT)
+                nc.vector.tensor_scalar_mul(out=side_gain[:], in0=gain[:], scalar1=SIDE_WEIGHT)
+            if finished:
+                fuse(finished, weighted)
+                finished = None
+            if next_group < len(groups) and last_round_of[next_group] <= step - LAG:
+                finished = multiply(groups[next_group])
+                next_group += 1
+        while True:
+            fuse(finished, weigh(finished))
+            if next_group == len(groups):
+                break
+            finished = multiply(groups[next_group])
+            next_group += 1
 
         shape = [P, CLIPS_PER_PARTITION, CLIP]
         top = keep.tile([P, CLIPS_PER_PARTITION], F32, name="top")
@@ -240,34 +308,19 @@ def tile_custommodel_pb_t_kernel(tc, te, fe_n, loc_n, glob_n, logit_scale, logit
             out=shifted[:], in0=logits[:], in1=top[:].unsqueeze(2).to_broadcast(shape), op=ALU.subtract
         )
         terms = keep.tile([P, 2] + shape[1:], F32, name="terms")
-        nc.scalar.activation(out=terms[:, 0], in_=shifted[:], func=ACT.Exp)
-        nc.vector.tensor_tensor(out=terms[:, 1], in0=terms[:, 0], in1=logits[:], op=ALU.mult)
-        totals = keep.tile([P, 2 * CLIPS_PER_PARTITION], F32, name="totals")
+        nc.scalar.activation(out=terms[:, 1], in_=shifted[:], func=ACT.Exp)
+        nc.vector.tensor_tensor(out=terms[:, 0], in0=terms[:, 1], in1=logits[:], op=ALU.mult)
         nc.vector.tensor_reduce(
-            out=totals[:], in_=terms[:].rearrange("p h c j -> p (h c) j"), axis=AXIS.X, op=ALU.add
+            out=pooled_parts[:, :, 0:CLIPS_PER_PARTITION], in_=terms[:], axis=AXIS.X, op=ALU.add
         )
 
-        wide = [P, FOLD, 2 * CLIPS_PER_PARTITION]
-        spread = keep.tile(wide, F32, name="spread")
+        turned = banks.tile([P, 2, P], F32, name="turned", tag="bank")
+        for h in range(2):
+            nc.tensor.transpose(turned[:, h, :], pooled_parts[:, h, :], identity[:])
+        inverse = keep.tile([CLIPS_PER_PARTITION, P], F32, name="inverse")
+        nc.vector.reciprocal(out=inverse[:], in_=turned[0:CLIPS_PER_PARTITION, 1, :])
+        pooled = keep.tile([CLIPS_PER_PARTITION, P], F32, name="pooled")
         nc.vector.tensor_tensor(
-            out=spread[:],
-            in0=totals[:].unsqueeze(1).to_broadcast(wide),
-            in1=place[:].unsqueeze(2).to_broadcast(wide),
-            op=ALU.mult,
+            out=pooled[:], in0=turned[0:CLIPS_PER_PARTITION, 0, :], in1=inverse[:], op=ALU.mult
         )
-        folded = banks.tile([P, FOLD, 2, CLIPS_PER_PARTITION], F32, name="folded", tag="bank")
-        nc.tensor.matmul(
-            out=folded[:].rearrange("p b h c -> p (b h c)"),
-            lhsT=gather[:].rearrange("p r m -> p (r m)"),
-            rhs=spread[:].rearrange("p b k -> p (b k)"),
-            start=True,
-            stop=True,
-        )
-        inverse = keep.tile([P, FOLD, CLIPS_PER_PARTITION], F32, name="inverse")
-        nc.vector.reciprocal(out=inverse[:], in_=folded[:, :, 0, :])
-        pooled = keep.tile([P, FOLD, CLIPS_PER_PARTITION], F32, name="pooled")
-        nc.vector.tensor_tensor(out=pooled[:], in0=folded[:, :, 1, :], in1=inverse[:], op=ALU.mult)
-        nc.sync.dma_start(
-            out=out.rearrange("o (m k) -> (o m) k", k=FOLD * CLIPS_PER_PARTITION),
-            in_=pooled[0:OUT_ROWS].rearrange("p b c -> p (b c)"),
-        )
+        nc.sync.dma_start(out=out.rearrange("o (c p) -> (o c) p", p=P), in_=pooled[:])

@@ -17,8 +17,8 @@ FRAMES = 4096
 FEATURES = 1024
 QUERIES = 128
 CLIP = 8
-MAIN_WEIGHT = 0.9
 SIDE_WEIGHT = 0.05
+MAIN_FACTORS = (16, 2)
 
 FLOPS = 2 * 3 * QUERIES * FRAMES * FEATURES
 
@@ -33,16 +33,17 @@ MX_BLOCKS = P // 8
 HALF_BLOCK = 16
 
 FE, LOC, GLOB = 0, 1, 2
-ORDER = (FE, LOC, GLOB)
+ORDER = (LOC, GLOB, FE)
 
 PSUM_BANKS = 8
-TRANSPOSE_BANKS = PSUM_BANKS - 2
+PRODUCT_BANKS = 2
 PAIR = 2
 AHEAD = 8
 ROUNDS = [PAIR] * 15 + [1, 1]
 GROUPS = [4] * 7 + [2, 1, 1]
-STEPPED_ROUNDS = 1
 LAG = 2
+TE_STEP = 1
+TE_AFTER = 1
 
 
 def split(counts):
@@ -67,41 +68,42 @@ def tile_custommodel_pb_t_kernel(tc, te, fe_n, loc_n, glob_n, logit_scale, logit
     with ExitStack() as ctx:
         keep = ctx.enter_context(tc.tile_pool(name="keep", bufs=1))
         frames = ctx.enter_context(tc.tile_pool(name="frames", bufs=3 * AHEAD))
-        ordered = ctx.enter_context(tc.tile_pool(name="ordered", bufs=4))
+        ordered = ctx.enter_context(tc.tile_pool(name="ordered", bufs=6))
         stage = ctx.enter_context(tc.tile_pool(name="stage", bufs=6))
-        packed = ctx.enter_context(tc.tile_pool(name="packed", bufs=15))
-        sums = ctx.enter_context(tc.tile_pool(name="sums", bufs=2))
-        banks = ctx.enter_context(tc.psum_pool(name="banks", bufs=TRANSPOSE_BANKS))
-        products = ctx.enter_context(tc.psum_pool(name="products", bufs=1))
+        packed = ctx.enter_context(tc.tile_pool(name="packed", bufs=12))
+        banks = ctx.enter_context(tc.psum_pool(name="banks", bufs=PSUM_BANKS - PRODUCT_BANKS))
+        products = ctx.enter_context(tc.psum_pool(name="products", bufs=PRODUCT_BANKS))
         ctx.enter_context(tc.manual_schedule())
 
         loaded = {}
 
-        def load(stream, step, piece=PAIR):
-            first, count = rounds[step][0], len(rounds[step])
-            x = frames.tile([P, count, FEATURES], BF16, name="x")
-            loaded[(stream, step)] = x
-            c, j = first // CLIP, first % CLIP
-            for n in range(0, count, piece):
-                m = min(count, n + piece)
-                nc.sync.dma_start(out=x[:, n:m, :], in_=streams[stream][:, c, j + n : j + m, :])
-
-        def reorder(out, rows):
-            nc.vector.tensor_copy(
-                out=out.rearrange("p (k u s i) -> p k u s i", u=HALVES, s=MX_BLOCKS, i=HALF_BLOCK),
-                in_=rows.rearrange("p (k s u i) -> p k u s i", u=HALVES, s=MX_BLOCKS, i=HALF_BLOCK),
+        def load(stream, step, first=0, count=None):
+            tiles = rounds[step]
+            if first == 0:
+                x = frames.tile([P, len(tiles), FEATURES], BF16, name="x")
+                loaded[(stream, step)] = x
+            m = first + (count or len(tiles))
+            c, j = tiles[0] // CLIP, tiles[0] % CLIP
+            nc.sync.dma_start(
+                out=loaded[(stream, step)][:, first:m, :], in_=streams[stream][:, c, j + first : j + m, :]
             )
 
-        def transpose_words(rows, ordered_words, bank):
-            words = rows.bitcast(F32)
+        def take_second(rows, second):
+            nc.vector.tensor_copy(
+                out=second.rearrange("p (k m v i) -> p k m v i", m=MX_BLOCKS // 2, v=HALVES, i=HALF_BLOCK),
+                in_=rows.rearrange("p (k v m e i) -> p e k m v i", v=HALVES, m=MX_BLOCKS // 2, e=2, i=HALF_BLOCK)[:, 1],
+            )
+
+        def mend_first(rows):
+            view = rows.rearrange("p (k v m e i) -> p v e k m i", v=HALVES, m=MX_BLOCKS // 2, e=2, i=HALF_BLOCK)
+            nc.vector.tensor_copy(out=view[:, 0, 1], in_=view[:, 1, 0])
+
+        def transpose_words(first, second, bank):
+            first_words = first.bitcast(F32)
+            second_words = second.bitcast(F32)
             for g in range(PASSES):
-                for u in range(HALVES):
-                    n = g * HALVES + u
-                    if ordered_words:
-                        half = words[:, n * P : (n + 1) * P]
-                    else:
-                        half = words[:, g * HALVES * P + u : (g + 1) * HALVES * P : HALVES]
-                    nc.tensor.transpose(bank[:, n, :], half, identity[:])
+                nc.tensor.transpose(bank[:, g * HALVES, :], first_words[:, g * HALVES * P : (g * HALVES + 1) * P], identity[:])
+                nc.tensor.transpose(bank[:, g * HALVES + 1, :], second_words[:, g * P : (g + 1) * P], identity[:])
 
         def regroup(copy, bank, grouped_rows):
             copy(
@@ -112,10 +114,11 @@ def tile_custommodel_pb_t_kernel(tc, te, fe_n, loc_n, glob_n, logit_scale, logit
         te_rows = keep.tile([P, FEATURES], BF16, name="te_rows")
         scale_raw = keep.tile([P, 1], BF16, name="scale_raw")
         bias_raw = keep.tile([P, 1], BF16, name="bias_raw")
-        load(ORDER[0], 0, 1)
-        nc.sync.dma_start(out=te_rows[:], in_=te)
-        for stream in ORDER[1:]:
-            load(stream, 0, 1)
+        first_pieces = [(stream, n) for stream in ORDER for n in range(len(rounds[0]))]
+        for i, (stream, n) in enumerate(first_pieces):
+            if i == TE_AFTER:
+                nc.sync.dma_start(out=te_rows[:], in_=te)
+            load(stream, 0, n, 1)
         nc.scalar.dma_start(out=scale_raw[:], in_=logit_scale.partition_broadcast(P))
         nc.scalar.dma_start(out=bias_raw[:], in_=logit_bias.partition_broadcast(P))
         for step in range(1, AHEAD):
@@ -126,57 +129,69 @@ def tile_custommodel_pb_t_kernel(tc, te, fe_n, loc_n, glob_n, logit_scale, logit
         make_identity(nc, identity[:])
         pooled_parts = keep.tile([P, 2, P], F32, name="pooled_parts")
         nc.gpsimd.memset(pooled_parts[:], 0.0)
-
         blank = keep.tile([P, 1], F32, name="blank")
         nc.gpsimd.memset(blank[:], 0.0)
         one = keep.tile([P, 1], F32, name="one")
         nc.scalar.activation(out=one[:], in_=blank[:], func=ACT.Exp)
         gain = keep.tile([P, 1], F32, name="gain")
+        bias = keep.tile([P, 1], F32, name="bias")
+        side_gain = keep.tile([P, 1], F32, name="side_gain")
 
+        te_multiples = {}
         te_codes = {}
         te_scales = {}
 
-        def prepare_te():
-            te_ordered = keep.tile([P, FEATURES], BF16, name="te_ordered")
-            reorder(te_ordered[:], te_rows[:])
-            for ordered_words, rows in ((True, te_ordered), (False, te_rows)):
-                te_bank = products.tile([P, WORD_BLOCKS, P], F32, name="te_bank", tag="main" if ordered_words else "side")
-                transpose_words(rows[:], ordered_words, te_bank)
-                te_grouped = keep.tile([P, FEATURES], BF16, name="te_grouped%d" % ordered_words, align_bytes=64)
-                regroup(nc.vector.tensor_copy, te_bank, te_grouped[:])
-                codes = keep.tile([P, PASSES * QUERIES], U32, name="te_codes%d" % ordered_words, align_bytes=64)
-                scales = keep.tile([P, PASSES * QUERIES], U8, name="te_scales%d" % ordered_words, align_bytes=64)
-                nc.vector.quantize_mx(out=codes[:].bitcast(FP8X4), scales=scales[:], in_=te_grouped[:])
-                te_codes[ordered_words] = codes
-                te_scales[ordered_words] = scales
+        def transpose_te():
+            te_second = keep.tile([P, FEATURES // HALVES], BF16, name="te_second")
+            take_second(te_rows[:], te_second[:])
+            mend_first(te_rows[:])
+            te_bank = products.tile([P, WORD_BLOCKS, P], F32, name="te_bank", tag="product")
+            transpose_words(te_rows[:], te_second[:], te_bank)
+            te_grouped = keep.tile([P, FEATURES], BF16, name="te_grouped", align_bytes=64)
+            regroup(nc.vector.tensor_copy, te_bank, te_grouped[:])
+            return te_grouped
 
-        bias = keep.tile([P, 1], F32, name="bias")
-        main_gain = keep.tile([P, 1], F32, name="main_gain")
-        side_gain = keep.tile([P, 1], F32, name="side_gain")
+        def scale_te(factor):
+            rows = keep.tile([P, FEATURES], BF16, name="te_times_%d" % factor, align_bytes=64)
+            nc.scalar.mul(rows[:], te_multiples[1][:], float(factor))
+            te_multiples[factor] = rows
+
+        def quantise_te(factor):
+            codes = keep.tile([P, PASSES * QUERIES], U32, name="te_codes_%d" % factor, align_bytes=64)
+            scales = keep.tile([P, PASSES * QUERIES], U8, name="te_scales_%d" % factor, align_bytes=64)
+            nc.vector.quantize_mx(out=codes[:].bitcast(FP8X4), scales=scales[:], in_=te_multiples[factor][:])
+            te_codes[factor] = codes
+            te_scales[factor] = scales
 
         logits = keep.tile([P, CLIPS_PER_PARTITION, CLIP], F32, name="logits")
+        flat_logits = logits[:].rearrange("p c j -> p (c j)")
 
-        def is_ordered(stream, step):
-            return stream != FE and step >= STEPPED_ROUNDS
+        second_of = {}
 
-        rows_of = {}
-
-        def reorder_rows(stream, step):
-            x = loaded[(stream, step)]
+        def pieces_of(step):
             count = len(rounds[step])
-            if is_ordered(stream, step):
-                r = ordered.tile([P, count, FEATURES], BF16, name="r")
-                reorder(r[:].rearrange("p t d -> p (t d)"), x[:].rearrange("p t d -> p (t d)"))
-                rows_of[(stream, step)] = r
-            else:
-                rows_of[(stream, step)] = x
+            piece = 1 if step == 0 else count
+            return [slice(n, n + piece) for n in range(0, count, piece)]
 
-        def transpose_rows(stream, step, vector_copies=()):
+        def flat(rows):
+            return rows.rearrange("p t d -> p (t d)")
+
+        def take_second_rows(stream, step):
+            second = ordered.tile([P, len(rounds[step]), FEATURES // HALVES], BF16, name="second")
+            second_of[(stream, step)] = second
+            for part in pieces_of(step):
+                take_second(flat(loaded[(stream, step)][:, part, :]), flat(second[:, part, :]))
+
+        def mend_first_rows(stream, step):
+            for part in pieces_of(step):
+                mend_first(flat(loaded[(stream, step)][:, part, :]))
+
+        def transpose_rows(stream, step, vector_copies):
             count = len(rounds[step])
             grouped = stage.tile([P, count * FEATURES], BF16, name="grouped", align_bytes=64)
             for n in range(count):
                 bank = banks.tile([P, WORD_BLOCKS, P], F32, name="bank")
-                transpose_words(rows_of[(stream, step)][:, n, :], is_ordered(stream, step), bank)
+                transpose_words(loaded[(stream, step)][:, n, :], second_of[(stream, step)][:, n, :], bank)
                 copy = nc.vector.tensor_copy if n in vector_copies else nc.scalar.copy
                 regroup(copy, bank, grouped[:, n * FEATURES : (n + 1) * FEATURES])
             if step + AHEAD < len(rounds):
@@ -191,114 +206,84 @@ def tile_custommodel_pb_t_kernel(tc, te, fe_n, loc_n, glob_n, logit_scale, logit
             scales = packed.tile([P, count * PASSES * P], U8, name="scales", align_bytes=64)
             nc.vector.quantize_mx(out=codes[:].bitcast(FP8X4), scales=scales[:], in_=grouped[:])
             for n, t in enumerate(rounds[step]):
-                quantised[(stream, t)] = (codes, scales, n, is_ordered(stream, step))
+                quantised[(stream, t)] = (codes, scales, n)
 
-        def multiply(group):
-            if len(group) == max(GROUPS):
-                side = products.tile([P, max(GROUPS) * QUERIES], F32, name="side")
-                main = products.tile([P, max(GROUPS) * QUERIES], F32, name="main")
-            else:
-                side = banks.tile([P, max(GROUPS) * QUERIES], F32, name="last_side", tag="bank")
-                main = banks.tile([P, max(GROUPS) * QUERIES], F32, name="last_main", tag="bank")
-            for j, t in enumerate(group):
-                for stream in (LOC, GLOB, FE):
-                    codes, scales, n, ordered_words = quantised[(stream, t)]
-                    product = main if stream == FE else side
-                    for g in range(PASSES):
-                        cols = slice((n * PASSES + g) * P, (n * PASSES + g + 1) * P)
-                        te_cols = slice(g * QUERIES, (g + 1) * QUERIES)
-                        nc.tensor.matmul_mx(
-                            out=product[:, j * QUERIES : (j + 1) * QUERIES],
-                            lhsT=codes[:, cols].bitcast(FP8X4),
-                            lhsT_scale=scales[:, cols],
-                            rhs=te_codes[ordered_words][:, te_cols].bitcast(FP8X4),
-                            rhs_scale=te_scales[ordered_words][:, te_cols],
-                            start=(stream != GLOB and g == 0),
-                            stop=(stream != LOC and g == PASSES - 1),
-                        )
-            return group, main, side
+        current = {}
 
-        def weigh(done):
-            group, main, side = done
-            weighted = sums.tile([P, max(GROUPS) * QUERIES], F32, name="weighted")
-            width = len(group) * QUERIES
-            nc.scalar.activation(
-                out=weighted[:, :width],
-                in_=side[:, :width],
-                func=ACT.Identity,
-                scale=side_gain[:, 0:1],
-                bias=bias[:, 0:1],
-            )
-            return weighted
+        def multiply(t):
+            group = group_of[t]
+            if t == group[0]:
+                product = products.tile([P, max(GROUPS), QUERIES], F32, name="product")
+                current["product"] = product
+            passes = [(stream, 1, g) for stream in (LOC, GLOB) for g in range(PASSES)]
+            passes += [(FE, factor, g) for factor in MAIN_FACTORS for g in range(PASSES)]
+            for i, (stream, factor, g) in enumerate(passes):
+                codes, scales, n = quantised[(stream, t)]
+                cols = slice((n * PASSES + g) * P, (n * PASSES + g + 1) * P)
+                te_cols = slice(g * QUERIES, (g + 1) * QUERIES)
+                nc.tensor.matmul_mx(
+                    out=current["product"][:, t - group[0], :],
+                    lhsT=codes[:, cols].bitcast(FP8X4),
+                    lhsT_scale=scales[:, cols],
+                    rhs=te_codes[factor][:, te_cols].bitcast(FP8X4),
+                    rhs_scale=te_scales[factor][:, te_cols],
+                    start=(i == 0),
+                    stop=(i == len(passes) - 1),
+                )
+            return (group, current["product"]) if t == group[-1] else None
 
-        def fuse(done, weighted):
-            group, main, side = done
-            width = len(group) * QUERIES
-            fused = sums.tile([P, max(GROUPS) * QUERIES], F32, name="fused")
-            nc.vector.scalar_tensor_tensor(
-                out=fused[:, :width],
-                in0=main[:, :width],
-                scalar=main_gain[:, 0:1],
-                in1=weighted[:, :width],
-                op0=ALU.mult,
-                op1=ALU.add,
-            )
-            nc.vector.tensor_reduce(
-                out=logits[:].rearrange("p c j -> p (c j)")[:, group[0] : group[-1] + 1],
-                in_=fused[:, :width].rearrange("p (t q) -> p t q", q=QUERIES),
-                axis=AXIS.X,
-                op=ALU.max,
-            )
+        def maximise(done):
+            group, product = done
+            cols = flat_logits[:, group[0] : group[-1] + 1]
+            nc.vector.tensor_reduce(out=cols, in_=product[:, : len(group), :], axis=AXIS.X, op=ALU.max)
 
         grouped_of = {}
-        finished = None
-        last_round_of = {}
-        for n, group in enumerate(groups):
-            last_round_of[n] = [i for i in range(len(rounds)) if group[-1] in rounds[i]][0]
+        finished = []
         for stream in ORDER:
-            reorder_rows(stream, 0)
-        next_group = 0
+            take_second_rows(stream, 0)
+            mend_first_rows(stream, 0)
         for step in range(len(rounds) + LAG):
-            weighted = None
             if step < len(rounds):
+                last = step >= len(rounds) - 2
                 for stream in ORDER:
-                    grouped_of[(stream, step)] = transpose_rows(
-                        stream, step, (len(rounds[step]) - 1,) if step >= len(rounds) - 2 and stream == LOC else ()
-                    )
-                    if stream == ORDER[0] and finished:
-                        weighted = weigh(finished)
-                    if stream == ORDER[0] and step == 0:
-                        prepare_te()
-                if step == 1:
-                    nc.scalar.activation(out=gain[:], in_=scale_raw[:], func=ACT.Exp)
-            elif finished:
-                weighted = weigh(finished)
-            ops = []
-            if 1 <= step <= len(rounds):
-                ops += [("q", stream) for stream in ORDER]
-            if step + 1 < len(rounds):
-                ops = ops[:1] + [("r", FE), ("r", LOC), ("r", GLOB)] + ops[1:]
-            for kind, stream in ops:
-                if kind == "q":
-                    quantise(stream, step - 1, grouped_of[(stream, step - 1)])
-                else:
-                    reorder_rows(stream, step + 1)
-            if step == 2:
+                    vector_copies = (0,) if last and stream == GLOB else ()
+                    grouped_of[(stream, step)] = transpose_rows(stream, step, vector_copies)
+                    if step == 0 and stream == ORDER[0]:
+                        te_multiples[1] = transpose_te()
+                if step == 0:
+                    for factor in MAIN_FACTORS:
+                        scale_te(factor)
+            if step == 1:
+                nc.scalar.activation(out=gain[:], in_=scale_raw[:], func=ACT.Exp)
                 nc.vector.tensor_copy(out=bias[:], in_=bias_raw[:])
-                nc.vector.tensor_scalar_mul(out=main_gain[:], in0=gain[:], scalar1=MAIN_WEIGHT)
+            if step == 2:
                 nc.vector.tensor_scalar_mul(out=side_gain[:], in0=gain[:], scalar1=SIDE_WEIGHT)
-            if finished:
-                fuse(finished, weighted)
-                finished = None
-            if next_group < len(groups) and last_round_of[next_group] <= step - LAG:
-                finished = multiply(groups[next_group])
-                next_group += 1
-        while True:
-            fuse(finished, weigh(finished))
-            if next_group == len(groups):
-                break
-            finished = multiply(groups[next_group])
-            next_group += 1
+            to_quantise = [s for s in ORDER if 1 <= step <= len(rounds)]
+            to_reorder = [s for s in ORDER if step + 1 < len(rounds)]
+            for i in range(len(ORDER)):
+                for stream in to_reorder[i : i + 1]:
+                    take_second_rows(stream, step + 1)
+                for stream in to_quantise[i : i + 1]:
+                    quantise(stream, step - 1, grouped_of[(stream, step - 1)])
+                for stream in to_reorder[i : i + 1]:
+                    mend_first_rows(stream, step + 1)
+            if step == TE_STEP:
+                for factor in (1,) + MAIN_FACTORS:
+                    quantise_te(factor)
+            for done in finished:
+                maximise(done)
+            finished = []
+            if step >= LAG:
+                for t in rounds[step - LAG]:
+                    done = multiply(t)
+                    if done:
+                        finished.append(done)
+        for done in finished:
+            maximise(done)
+
+        nc.vector.tensor_scalar(
+            out=flat_logits, in0=flat_logits, scalar1=side_gain[:, 0:1], scalar2=bias[:, 0:1], op0=ALU.mult, op1=ALU.add
+        )
 
         shape = [P, CLIPS_PER_PARTITION, CLIP]
         top = keep.tile([P, CLIPS_PER_PARTITION], F32, name="top")

@@ -42,6 +42,7 @@ AHEAD = 8
 ROUNDS = [PAIR] * 15 + [1, 1]
 GROUPS = [4] * 7 + [2, 1, 1]
 LAG = 2
+RUN = 3
 TE_STEP = 1
 TE_AFTER = 1
 
@@ -186,7 +187,7 @@ def tile_custommodel_pb_t_kernel(tc, te, fe_n, loc_n, glob_n, logit_scale, logit
             for part in pieces_of(step):
                 mend_first(flat(loaded[(stream, step)][:, part, :]))
 
-        def transpose_rows(stream, step, vector_copies):
+        def transpose_rows(stream, step, vector_copies, after_tile):
             count = len(rounds[step])
             grouped = stage.tile([P, count * FEATURES], BF16, name="grouped", align_bytes=64)
             for n in range(count):
@@ -194,6 +195,7 @@ def tile_custommodel_pb_t_kernel(tc, te, fe_n, loc_n, glob_n, logit_scale, logit
                 transpose_words(loaded[(stream, step)][:, n, :], second_of[(stream, step)][:, n, :], bank)
                 copy = nc.vector.tensor_copy if n in vector_copies else nc.scalar.copy
                 regroup(copy, bank, grouped[:, n * FEATURES : (n + 1) * FEATURES])
+                after_tile()
             if step + AHEAD < len(rounds):
                 load(stream, step + AHEAD)
             return grouped
@@ -243,11 +245,26 @@ def tile_custommodel_pb_t_kernel(tc, te, fe_n, loc_n, glob_n, logit_scale, logit
             take_second_rows(stream, 0)
             mend_first_rows(stream, 0)
         for step in range(len(rounds) + LAG):
+            to_multiply = list(rounds[step - LAG]) if step >= LAG else []
+            transposed = []
+
+            def after_tile():
+                transposed.append(1)
+                if len(transposed) % RUN == 0 and len(transposed) < len(ORDER) * PAIR and to_multiply:
+                    multiply_next()
+
+            def multiply_next():
+                t = to_multiply[0]
+                to_multiply.remove(t)
+                done = multiply(t)
+                if done:
+                    finished.append(done)
+
             if step < len(rounds):
                 last = step >= len(rounds) - 2
                 for stream in ORDER:
                     vector_copies = (0,) if last and stream == GLOB else ()
-                    grouped_of[(stream, step)] = transpose_rows(stream, step, vector_copies)
+                    grouped_of[(stream, step)] = transpose_rows(stream, step, vector_copies, after_tile)
                     if step == 0 and stream == ORDER[0]:
                         te_multiples[1] = transpose_te()
                 if step == 0:
@@ -272,12 +289,9 @@ def tile_custommodel_pb_t_kernel(tc, te, fe_n, loc_n, glob_n, logit_scale, logit
                     quantise_te(factor)
             for done in finished:
                 maximise(done)
-            finished = []
-            if step >= LAG:
-                for t in rounds[step - LAG]:
-                    done = multiply(t)
-                    if done:
-                        finished.append(done)
+            finished.clear()
+            while to_multiply:
+                multiply_next()
         for done in finished:
             maximise(done)
 

@@ -33,7 +33,6 @@ MX_BLOCKS = P // 8
 HALF_BLOCK = 16
 
 FE, LOC, GLOB = 0, 1, 2
-ORDER = (LOC, GLOB, FE)
 
 PSUM_BANKS = 8
 PRODUCT_BANKS = 2
@@ -42,9 +41,14 @@ AHEAD = 8
 ROUNDS = [PAIR] * 15 + [1, 1]
 GROUPS = [4] * 7 + [2, 1, 1]
 LAG = 2
-RUN = 3
+TE_FORMS = [(True, 1), (False, 1), (False, 16), (False, 2)]
+EARLY_CLIPS = 3
 TE_STEP = 1
 TE_AFTER = 1
+
+
+def order(step):
+    return (LOC, GLOB, FE) if step >= len(ROUNDS) - 2 else (FE, LOC, GLOB)
 
 
 def split(counts):
@@ -100,11 +104,17 @@ def tile_custommodel_pb_t_kernel(tc, te, fe_n, loc_n, glob_n, logit_scale, logit
             nc.vector.tensor_copy(out=view[:, 0, 1], in_=view[:, 1, 0])
 
         def transpose_words(first, second, bank):
-            first_words = first.bitcast(F32)
-            second_words = second.bitcast(F32)
+            words = first.bitcast(F32)
             for g in range(PASSES):
-                nc.tensor.transpose(bank[:, g * HALVES, :], first_words[:, g * HALVES * P : (g * HALVES + 1) * P], identity[:])
-                nc.tensor.transpose(bank[:, g * HALVES + 1, :], second_words[:, g * P : (g + 1) * P], identity[:])
+                for u in range(HALVES):
+                    start = g * HALVES * P
+                    if not second:
+                        run = words[:, start + u : start + HALVES * P : HALVES]
+                    elif u == 0:
+                        run = words[:, start : start + P]
+                    else:
+                        run = second[0].bitcast(F32)[:, g * P : (g + 1) * P]
+                    nc.tensor.transpose(bank[:, g * HALVES + u, :], run, identity[:])
 
         def regroup(copy, bank, grouped_rows):
             copy(
@@ -115,7 +125,7 @@ def tile_custommodel_pb_t_kernel(tc, te, fe_n, loc_n, glob_n, logit_scale, logit
         te_rows = keep.tile([P, FEATURES], BF16, name="te_rows")
         scale_raw = keep.tile([P, 1], BF16, name="scale_raw")
         bias_raw = keep.tile([P, 1], BF16, name="bias_raw")
-        first_pieces = [(stream, n) for stream in ORDER for n in range(len(rounds[0]))]
+        first_pieces = [(stream, n) for stream in order(0) for n in range(len(rounds[0]))]
         for i, (stream, n) in enumerate(first_pieces):
             if i == TE_AFTER:
                 nc.sync.dma_start(out=te_rows[:], in_=te)
@@ -123,7 +133,7 @@ def tile_custommodel_pb_t_kernel(tc, te, fe_n, loc_n, glob_n, logit_scale, logit
         nc.scalar.dma_start(out=scale_raw[:], in_=logit_scale.partition_broadcast(P))
         nc.scalar.dma_start(out=bias_raw[:], in_=logit_bias.partition_broadcast(P))
         for step in range(1, AHEAD):
-            for stream in ORDER:
+            for stream in order(step):
                 load(stream, step)
 
         identity = keep.tile([P, P], F32, name="identity")
@@ -142,30 +152,38 @@ def tile_custommodel_pb_t_kernel(tc, te, fe_n, loc_n, glob_n, logit_scale, logit
         te_codes = {}
         te_scales = {}
 
-        def transpose_te():
-            te_second = keep.tile([P, FEATURES // HALVES], BF16, name="te_second")
-            take_second(te_rows[:], te_second[:])
-            mend_first(te_rows[:])
+        def transpose_te(exchanged, copy):
+            second = []
+            if exchanged:
+                te_second = keep.tile([P, FEATURES // HALVES], BF16, name="te_second")
+                take_second(te_rows[:], te_second[:])
+                mend_first(te_rows[:])
+                second = [te_second[:]]
             te_bank = products.tile([P, WORD_BLOCKS, P], F32, name="te_bank", tag="product")
-            transpose_words(te_rows[:], te_second[:], te_bank)
-            te_grouped = keep.tile([P, FEATURES], BF16, name="te_grouped", align_bytes=64)
-            regroup(nc.vector.tensor_copy, te_bank, te_grouped[:])
-            return te_grouped
+            transpose_words(te_rows[:], second, te_bank)
+            te_grouped = keep.tile([P, FEATURES], BF16, name="te_grouped_%d" % exchanged, align_bytes=64)
+            regroup(copy, te_bank, te_grouped[:])
+            te_multiples[(exchanged, 1)] = te_grouped
 
-        def scale_te(factor):
-            rows = keep.tile([P, FEATURES], BF16, name="te_times_%d" % factor, align_bytes=64)
-            nc.scalar.mul(rows[:], te_multiples[1][:], float(factor))
-            te_multiples[factor] = rows
+        def scale_te(exchanged, factor):
+            rows = keep.tile([P, FEATURES], BF16, name="te_%d_times_%d" % (exchanged, factor), align_bytes=64)
+            nc.scalar.mul(rows[:], te_multiples[(exchanged, 1)][:], float(factor))
+            te_multiples[(exchanged, factor)] = rows
 
-        def quantise_te(factor):
-            codes = keep.tile([P, PASSES * QUERIES], U32, name="te_codes_%d" % factor, align_bytes=64)
-            scales = keep.tile([P, PASSES * QUERIES], U8, name="te_scales_%d" % factor, align_bytes=64)
-            nc.vector.quantize_mx(out=codes[:].bitcast(FP8X4), scales=scales[:], in_=te_multiples[factor][:])
-            te_codes[factor] = codes
-            te_scales[factor] = scales
+        def quantise_te(exchanged, factor):
+            codes = keep.tile([P, PASSES * QUERIES], U32, name="te_codes_%d_%d" % (exchanged, factor), align_bytes=64)
+            scales = keep.tile([P, PASSES * QUERIES], U8, name="te_scales_%d_%d" % (exchanged, factor), align_bytes=64)
+            rows = te_multiples[(exchanged, factor)]
+            nc.vector.quantize_mx(out=codes[:].bitcast(FP8X4), scales=scales[:], in_=rows[:])
+            te_codes[(exchanged, factor)] = codes
+            te_scales[(exchanged, factor)] = scales
 
+        peaks = keep.tile([P, CLIPS_PER_PARTITION, CLIP], F32, name="peaks")
+        flat_peaks = peaks[:].rearrange("p c j -> p (c j)")
         logits = keep.tile([P, CLIPS_PER_PARTITION, CLIP], F32, name="logits")
-        flat_logits = logits[:].rearrange("p c j -> p (c j)")
+
+        def is_exchanged(stream, step):
+            return stream != FE and step < len(rounds) - 2
 
         second_of = {}
 
@@ -178,26 +196,28 @@ def tile_custommodel_pb_t_kernel(tc, te, fe_n, loc_n, glob_n, logit_scale, logit
             return rows.rearrange("p t d -> p (t d)")
 
         def take_second_rows(stream, step):
+            if not is_exchanged(stream, step):
+                return
             second = ordered.tile([P, len(rounds[step]), FEATURES // HALVES], BF16, name="second")
             second_of[(stream, step)] = second
             for part in pieces_of(step):
                 take_second(flat(loaded[(stream, step)][:, part, :]), flat(second[:, part, :]))
 
         def mend_first_rows(stream, step):
+            if not is_exchanged(stream, step):
+                return
             for part in pieces_of(step):
                 mend_first(flat(loaded[(stream, step)][:, part, :]))
 
-        def transpose_rows(stream, step, vector_copies, after_tile):
+        def transpose_rows(stream, step, vector_copies):
             count = len(rounds[step])
             grouped = stage.tile([P, count * FEATURES], BF16, name="grouped", align_bytes=64)
             for n in range(count):
                 bank = banks.tile([P, WORD_BLOCKS, P], F32, name="bank")
-                transpose_words(loaded[(stream, step)][:, n, :], second_of[(stream, step)][:, n, :], bank)
+                second = [second_of[(stream, step)][:, n, :]] if is_exchanged(stream, step) else []
+                transpose_words(loaded[(stream, step)][:, n, :], second, bank)
                 copy = nc.vector.tensor_copy if n in vector_copies else nc.scalar.copy
                 regroup(copy, bank, grouped[:, n * FEATURES : (n + 1) * FEATURES])
-                after_tile()
-            if step + AHEAD < len(rounds):
-                load(stream, step + AHEAD)
             return grouped
 
         quantised = {}
@@ -208,7 +228,7 @@ def tile_custommodel_pb_t_kernel(tc, te, fe_n, loc_n, glob_n, logit_scale, logit
             scales = packed.tile([P, count * PASSES * P], U8, name="scales", align_bytes=64)
             nc.vector.quantize_mx(out=codes[:].bitcast(FP8X4), scales=scales[:], in_=grouped[:])
             for n, t in enumerate(rounds[step]):
-                quantised[(stream, t)] = (codes, scales, n)
+                quantised[(stream, t)] = (codes, scales, n, is_exchanged(stream, step))
 
         current = {}
 
@@ -220,15 +240,15 @@ def tile_custommodel_pb_t_kernel(tc, te, fe_n, loc_n, glob_n, logit_scale, logit
             passes = [(stream, 1, g) for stream in (LOC, GLOB) for g in range(PASSES)]
             passes += [(FE, factor, g) for factor in MAIN_FACTORS for g in range(PASSES)]
             for i, (stream, factor, g) in enumerate(passes):
-                codes, scales, n = quantised[(stream, t)]
+                codes, scales, n, exchanged = quantised[(stream, t)]
                 cols = slice((n * PASSES + g) * P, (n * PASSES + g + 1) * P)
                 te_cols = slice(g * QUERIES, (g + 1) * QUERIES)
                 nc.tensor.matmul_mx(
                     out=current["product"][:, t - group[0], :],
                     lhsT=codes[:, cols].bitcast(FP8X4),
                     lhsT_scale=scales[:, cols],
-                    rhs=te_codes[factor][:, te_cols].bitcast(FP8X4),
-                    rhs_scale=te_scales[factor][:, te_cols],
+                    rhs=te_codes[(exchanged, factor)][:, te_cols].bitcast(FP8X4),
+                    rhs_scale=te_scales[(exchanged, factor)][:, te_cols],
                     start=(i == 0),
                     stop=(i == len(passes) - 1),
                 )
@@ -236,82 +256,143 @@ def tile_custommodel_pb_t_kernel(tc, te, fe_n, loc_n, glob_n, logit_scale, logit
 
         def maximise(done):
             group, product = done
-            cols = flat_logits[:, group[0] : group[-1] + 1]
+            cols = flat_peaks[:, group[0] : group[-1] + 1]
             nc.vector.tensor_reduce(out=cols, in_=product[:, : len(group), :], axis=AXIS.X, op=ALU.max)
+
+        def weigh(clips):
+            nc.vector.tensor_scalar(
+                out=logits[:, clips, :],
+                in0=peaks[:, clips, :],
+                scalar1=side_gain[:, 0:1],
+                scalar2=bias[:, 0:1],
+                op0=ALU.mult,
+                op1=ALU.add,
+            )
+
+        terms = keep.tile([P, 2, CLIPS_PER_PARTITION, CLIP], F32, name="terms")
+        top = keep.tile([P, CLIPS_PER_PARTITION], F32, name="top")
+        shifted = keep.tile([P, CLIPS_PER_PARTITION, CLIP], F32, name="shifted")
+
+        def shift_early():
+            clips = slice(0, EARLY_CLIPS)
+            shape = [P, EARLY_CLIPS, CLIP]
+            nc.vector.tensor_reduce(out=top[:, clips], in_=peaks[:, clips, :], axis=AXIS.X, op=ALU.max)
+            nc.vector.tensor_tensor(
+                out=shifted[:, clips, :],
+                in0=peaks[:, clips, :],
+                in1=top[:, clips].unsqueeze(2).to_broadcast(shape),
+                op=ALU.subtract,
+            )
+            weigh(clips)
+
+        def exponentiate_early():
+            clips = slice(0, EARLY_CLIPS)
+            nc.scalar.activation(
+                out=terms[:, 1, clips, :], in_=shifted[:, clips, :], func=ACT.Exp, scale=side_gain[:, 0:1]
+            )
+
+        def sum_early():
+            clips = slice(0, EARLY_CLIPS)
+            nc.vector.tensor_tensor(
+                out=terms[:, 0, clips, :], in0=terms[:, 1, clips, :], in1=logits[:, clips, :], op=ALU.mult
+            )
+            nc.vector.tensor_reduce(
+                out=pooled_parts[:, :, clips], in_=terms[:, :, clips, :], axis=AXIS.X, op=ALU.add
+            )
+
+        def pool_last():
+            c = EARLY_CLIPS
+            nc.vector.tensor_reduce(out=top[:, c : c + 1], in_=peaks[:, c, :], axis=AXIS.X, op=ALU.max)
+            nc.vector.tensor_scalar(
+                out=shifted[:, c, :], in0=peaks[:, c, :], scalar1=top[:, c : c + 1], scalar2=None, op0=ALU.subtract
+            )
+            nc.scalar.activation(
+                out=terms[:, 1, c, :],
+                in_=shifted[:, c, :],
+                func=ACT.Exp,
+                scale=side_gain[:, 0:1],
+                accum_out=pooled_parts[:, 1, c : c + 1],
+            )
+            weigh(slice(c, c + 1))
+            nc.vector.scalar_tensor_tensor(
+                out=terms[:, 0, c, :],
+                in0=terms[:, 1, c, :],
+                scalar=1.0,
+                in1=logits[:, c, :],
+                op0=ALU.mult,
+                op1=ALU.mult,
+                accum_out=pooled_parts[:, 0, c : c + 1],
+            )
 
         grouped_of = {}
         finished = []
-        for stream in ORDER:
+        to_multiply = []
+        pool_step = len(rounds) + LAG
+
+        def multiply_next():
+            t = to_multiply[0]
+            to_multiply.remove(t)
+            done = multiply(t)
+            if done:
+                finished.append(done)
+
+        for stream in order(0):
             take_second_rows(stream, 0)
             mend_first_rows(stream, 0)
         for step in range(len(rounds) + LAG):
-            to_multiply = list(rounds[step - LAG]) if step >= LAG else []
-            transposed = []
-
-            def after_tile():
-                transposed.append(1)
-                if len(transposed) % RUN == 0 and len(transposed) < len(ORDER) * PAIR and to_multiply:
-                    multiply_next()
-
-            def multiply_next():
-                t = to_multiply[0]
-                to_multiply.remove(t)
-                done = multiply(t)
-                if done:
-                    finished.append(done)
-
-            if step < len(rounds):
-                last = step >= len(rounds) - 2
-                for stream in ORDER:
-                    vector_copies = (0,) if last and stream == GLOB else ()
-                    grouped_of[(stream, step)] = transpose_rows(stream, step, vector_copies, after_tile)
-                    if step == 0 and stream == ORDER[0]:
-                        te_multiples[1] = transpose_te()
-                if step == 0:
-                    for factor in MAIN_FACTORS:
-                        scale_te(factor)
-            if step == 1:
-                nc.scalar.activation(out=gain[:], in_=scale_raw[:], func=ACT.Exp)
-                nc.vector.tensor_copy(out=bias[:], in_=bias_raw[:])
-            if step == 2:
-                nc.vector.tensor_scalar_mul(out=side_gain[:], in0=gain[:], scalar1=SIDE_WEIGHT)
-            to_quantise = [s for s in ORDER if 1 <= step <= len(rounds)]
-            to_reorder = [s for s in ORDER if step + 1 < len(rounds)]
-            for i in range(len(ORDER)):
-                for stream in to_reorder[i : i + 1]:
-                    take_second_rows(stream, step + 1)
-                for stream in to_quantise[i : i + 1]:
-                    quantise(stream, step - 1, grouped_of[(stream, step - 1)])
-                for stream in to_reorder[i : i + 1]:
-                    mend_first_rows(stream, step + 1)
+            to_quantise = [(s, step - 1) for s in order(step - 1)] if 1 <= step <= len(rounds) else []
+            to_exchange = [(s, step + 1) for s in order(step + 1)] if 1 <= step < len(rounds) - 1 else []
+            for i in range(len(streams)):
+                for rows in to_exchange[i : i + 1]:
+                    take_second_rows(*rows)
+                for rows in to_quantise[i : i + 1]:
+                    quantise(rows[0], rows[1], grouped_of[rows])
+                for rows in to_exchange[i : i + 1]:
+                    mend_first_rows(*rows)
             if step == TE_STEP:
-                for factor in (1,) + MAIN_FACTORS:
-                    quantise_te(factor)
+                for exchanged, factor in TE_FORMS:
+                    quantise_te(exchanged, factor)
+            if step == 3:
+                nc.vector.tensor_copy(out=bias[:], in_=bias_raw[:])
+                nc.vector.tensor_scalar_mul(out=side_gain[:], in0=gain[:], scalar1=SIDE_WEIGHT)
             for done in finished:
                 maximise(done)
+                if done[0][-1] == EARLY_CLIPS * CLIP - 1:
+                    pool_step = step
             finished.clear()
+            if step == pool_step:
+                shift_early()
+            if step == pool_step + 1:
+                sum_early()
+
+            if step >= LAG:
+                to_multiply.extend(rounds[step - LAG])
+            if step < len(rounds):
+                for stream in order(step):
+                    vector_copies = ()
+                    grouped_of[(stream, step)] = transpose_rows(stream, step, vector_copies)
+                    if step == 0 and stream == FE:
+                        transpose_te(False, nc.vector.tensor_copy)
+                        transpose_te(True, nc.vector.tensor_copy)
+                if step + AHEAD < len(rounds):
+                    for stream in order(step + AHEAD):
+                        load(stream, step + AHEAD)
+            if step == 0:
+                for exchanged, factor in TE_FORMS:
+                    if factor != 1:
+                        scale_te(exchanged, factor)
+                for stream in order(1):
+                    take_second_rows(stream, 1)
+                    mend_first_rows(stream, 1)
+            if step == pool_step:
+                exponentiate_early()
+            if step == 1:
+                nc.scalar.activation(out=gain[:], in_=scale_raw[:], func=ACT.Exp)
             while to_multiply:
                 multiply_next()
         for done in finished:
             maximise(done)
-
-        nc.vector.tensor_scalar(
-            out=flat_logits, in0=flat_logits, scalar1=side_gain[:, 0:1], scalar2=bias[:, 0:1], op0=ALU.mult, op1=ALU.add
-        )
-
-        shape = [P, CLIPS_PER_PARTITION, CLIP]
-        top = keep.tile([P, CLIPS_PER_PARTITION], F32, name="top")
-        nc.vector.tensor_reduce(out=top[:], in_=logits[:], axis=AXIS.X, op=ALU.max)
-        shifted = keep.tile(shape, F32, name="shifted")
-        nc.vector.tensor_tensor(
-            out=shifted[:], in0=logits[:], in1=top[:].unsqueeze(2).to_broadcast(shape), op=ALU.subtract
-        )
-        terms = keep.tile([P, 2] + shape[1:], F32, name="terms")
-        nc.scalar.activation(out=terms[:, 1], in_=shifted[:], func=ACT.Exp)
-        nc.vector.tensor_tensor(out=terms[:, 0], in0=terms[:, 1], in1=logits[:], op=ALU.mult)
-        nc.vector.tensor_reduce(
-            out=pooled_parts[:, :, 0:CLIPS_PER_PARTITION], in_=terms[:], axis=AXIS.X, op=ALU.add
-        )
+        pool_last()
 
         turned = banks.tile([P, 2, P], F32, name="turned", tag="bank")
         for h in range(2):

@@ -42,13 +42,20 @@ ROUNDS = [PAIR] * 15 + [1, 1]
 GROUPS = [4] * 7 + [2, 1, 1]
 LAG = 2
 TE_FORMS = [(True, 1), (False, 1), (False, 16), (False, 2)]
+VORDER = [("q", 0), ("q", 1), ("t", 0), ("q", 2), ("m", 0), ("t", 1), ("m", 1), ("t", 2), ("m", 2)]
+OSTEP = 1
+EXPAT = 2
+FIRST = 1
+LASTS = 2
+VTAIL = 1
+VT = 1
 EARLY_CLIPS = 3
 TE_STEP = 1
 TE_AFTER = 1
 
 
 def order(step):
-    return (LOC, GLOB, FE) if step >= len(ROUNDS) - 2 else (FE, LOC, GLOB)
+    return (LOC, GLOB, FE) if step >= OSTEP else (FE, LOC, GLOB)
 
 
 def split(counts):
@@ -167,7 +174,14 @@ def tile_custommodel_pb_t_kernel(tc, te, fe_n, loc_n, glob_n, logit_scale, logit
 
         def scale_te(exchanged, factor):
             rows = keep.tile([P, FEATURES], BF16, name="te_%d_times_%d" % (exchanged, factor), align_bytes=64)
-            nc.scalar.mul(rows[:], te_multiples[(exchanged, 1)][:], float(factor))
+            nc.gpsimd.tensor_scalar(
+                out=rows[:],
+                in0=te_multiples[(exchanged, 1)][:],
+                scalar1=float(factor),
+                scalar2=0.0,
+                op0=ALU.mult,
+                op1=ALU.add,
+            )
             te_multiples[(exchanged, factor)] = rows
 
         def quantise_te(exchanged, factor):
@@ -183,7 +197,7 @@ def tile_custommodel_pb_t_kernel(tc, te, fe_n, loc_n, glob_n, logit_scale, logit
         logits = keep.tile([P, CLIPS_PER_PARTITION, CLIP], F32, name="logits")
 
         def is_exchanged(stream, step):
-            return stream != FE and step < len(rounds) - 2
+            return stream != FE and FIRST <= step < len(rounds) - LASTS
 
         second_of = {}
 
@@ -342,13 +356,16 @@ def tile_custommodel_pb_t_kernel(tc, te, fe_n, loc_n, glob_n, logit_scale, logit
         for step in range(len(rounds) + LAG):
             to_quantise = [(s, step - 1) for s in order(step - 1)] if 1 <= step <= len(rounds) else []
             to_exchange = [(s, step + 1) for s in order(step + 1)] if 1 <= step < len(rounds) - 1 else []
-            for i in range(len(streams)):
-                for rows in to_exchange[i : i + 1]:
-                    take_second_rows(*rows)
-                for rows in to_quantise[i : i + 1]:
-                    quantise(rows[0], rows[1], grouped_of[rows])
-                for rows in to_exchange[i : i + 1]:
-                    mend_first_rows(*rows)
+            for kind, i in VORDER:
+                if kind == "q":
+                    for rows in to_quantise[i : i + 1]:
+                        quantise(rows[0], rows[1], grouped_of[rows])
+                elif kind == "t":
+                    for rows in to_exchange[i : i + 1]:
+                        take_second_rows(*rows)
+                else:
+                    for rows in to_exchange[i : i + 1]:
+                        mend_first_rows(*rows)
             if step == TE_STEP:
                 for exchanged, factor in TE_FORMS:
                     quantise_te(exchanged, factor)
@@ -369,11 +386,13 @@ def tile_custommodel_pb_t_kernel(tc, te, fe_n, loc_n, glob_n, logit_scale, logit
                 to_multiply.extend(rounds[step - LAG])
             if step < len(rounds):
                 for stream in order(step):
-                    vector_copies = ()
+                    vector_copies = (0,) if step >= len(rounds) - VTAIL and stream == order(step)[VT] else ()
                     grouped_of[(stream, step)] = transpose_rows(stream, step, vector_copies)
                     if step == 0 and stream == FE:
                         transpose_te(False, nc.vector.tensor_copy)
                         transpose_te(True, nc.vector.tensor_copy)
+                    if step == pool_step and stream == order(step)[EXPAT]:
+                        exponentiate_early()
                 if step + AHEAD < len(rounds):
                     for stream in order(step + AHEAD):
                         load(stream, step + AHEAD)
@@ -384,8 +403,6 @@ def tile_custommodel_pb_t_kernel(tc, te, fe_n, loc_n, glob_n, logit_scale, logit
                 for stream in order(1):
                     take_second_rows(stream, 1)
                     mend_first_rows(stream, 1)
-            if step == pool_step:
-                exponentiate_early()
             if step == 1:
                 nc.scalar.activation(out=gain[:], in_=scale_raw[:], func=ACT.Exp)
             while to_multiply:

@@ -42,12 +42,17 @@ ROUNDS = [PAIR] * 15 + [1, 1]
 GROUPS = [4] * 7 + [2, 1, 1]
 LAG = 2
 TE_FORMS = [(True, 1), (False, 1), (False, 16), (False, 2)]
-VORDER = [("q", 0), ("q", 1), ("t", 0), ("q", 2), ("m", 0), ("t", 1), ("m", 1), ("t", 2), ("m", 2)]
+VORDER = [("q", 0), ("t", 0), ("q", 1), ("m", 0), ("t", 1), ("m", 1), ("t", 2), ("m", 2)]
 OSTEP = 1
 EXPAT = 2
 FIRST = 1
-LASTS = 2
-VTAIL = 1
+JOIN = 2
+LASTS = 1
+CATCH = 100
+LATE = 1
+FREEBANKS = True
+DEFER = 15
+VTAIL = 0
 VT = 1
 EARLY_CLIPS = 3
 TE_STEP = 1
@@ -81,8 +86,8 @@ def tile_custommodel_pb_t_kernel(tc, te, fe_n, loc_n, glob_n, logit_scale, logit
         keep = ctx.enter_context(tc.tile_pool(name="keep", bufs=1))
         frames = ctx.enter_context(tc.tile_pool(name="frames", bufs=3 * AHEAD))
         ordered = ctx.enter_context(tc.tile_pool(name="ordered", bufs=6))
-        stage = ctx.enter_context(tc.tile_pool(name="stage", bufs=6))
-        packed = ctx.enter_context(tc.tile_pool(name="packed", bufs=12))
+        stage = ctx.enter_context(tc.tile_pool(name="stage", bufs=3))
+        packed = ctx.enter_context(tc.tile_pool(name="packed", bufs=4))
         banks = ctx.enter_context(tc.psum_pool(name="banks", bufs=PSUM_BANKS - PRODUCT_BANKS))
         products = ctx.enter_context(tc.psum_pool(name="products", bufs=PRODUCT_BANKS))
         ctx.enter_context(tc.manual_schedule())
@@ -223,33 +228,50 @@ def tile_custommodel_pb_t_kernel(tc, te, fe_n, loc_n, glob_n, logit_scale, logit
             for part in pieces_of(step):
                 mend_first(flat(loaded[(stream, step)][:, part, :]))
 
+        def joined(step):
+            names = order(step)
+            return [names[:JOIN]] + [names[i : i + 1] for i in range(JOIN, len(names))]
+
         def transpose_rows(stream, step, vector_copies):
             count = len(rounds[step])
-            grouped = stage.tile([P, count * FEATURES], BF16, name="grouped", align_bytes=64)
+            part = [names for names in joined(step) if stream in names][0]
+            if stream == part[0]:
+                grouped = stage.tile(
+                    [P, len(part) * count * FEATURES], BF16, name="grouped%d" % len(part), align_bytes=64
+                )
+                grouped_of[(part, step)] = grouped
+            first = part.index(stream) * count
             for n in range(count):
                 bank = banks.tile([P, WORD_BLOCKS, P], F32, name="bank")
                 second = [second_of[(stream, step)][:, n, :]] if is_exchanged(stream, step) else []
                 transpose_words(loaded[(stream, step)][:, n, :], second, bank)
                 copy = nc.vector.tensor_copy if n in vector_copies else nc.scalar.copy
-                regroup(copy, bank, grouped[:, n * FEATURES : (n + 1) * FEATURES])
-            return grouped
+                cols = slice((first + n) * FEATURES, (first + n + 1) * FEATURES)
+                regroup(copy, bank, grouped_of[(part, step)][:, cols])
 
         quantised = {}
 
-        def quantise(stream, step, grouped):
+        def quantise(part, step):
             count = len(rounds[step])
-            codes = packed.tile([P, count * PASSES * P], U32, name="codes", align_bytes=64)
-            scales = packed.tile([P, count * PASSES * P], U8, name="scales", align_bytes=64)
-            nc.vector.quantize_mx(out=codes[:].bitcast(FP8X4), scales=scales[:], in_=grouped[:])
-            for n, t in enumerate(rounds[step]):
-                quantised[(stream, t)] = (codes, scales, n, is_exchanged(stream, step))
+            width = len(part) * count * PASSES * P
+            codes = packed.tile([P, width], U32, name="codes%d" % len(part), align_bytes=64)
+            scales = packed.tile([P, width], U8, name="scales%d" % len(part), align_bytes=64)
+            nc.vector.quantize_mx(
+                out=codes[:].bitcast(FP8X4), scales=scales[:], in_=grouped_of[(part, step)][:]
+            )
+            for i, stream in enumerate(part):
+                for n, t in enumerate(rounds[step]):
+                    quantised[(stream, t)] = (codes, scales, i * count + n, is_exchanged(stream, step))
 
         current = {}
 
         def multiply(t):
             group = group_of[t]
             if t == group[0]:
-                product = products.tile([P, max(GROUPS), QUERIES], F32, name="product")
+                if len(group) == max(GROUPS) or not FREEBANKS:
+                    product = products.tile([P, max(GROUPS), QUERIES], F32, name="product")
+                else:
+                    product = banks.tile([P, max(GROUPS), QUERIES], F32, name="last_product", tag="bank")
                 current["product"] = product
             passes = [(stream, 1, g) for stream in (LOC, GLOB) for g in range(PASSES)]
             passes += [(FE, factor, g) for factor in MAIN_FACTORS for g in range(PASSES)]
@@ -341,6 +363,7 @@ def tile_custommodel_pb_t_kernel(tc, te, fe_n, loc_n, glob_n, logit_scale, logit
         grouped_of = {}
         finished = []
         to_multiply = []
+        multiplied = 0
         pool_step = len(rounds) + LAG
 
         def multiply_next():
@@ -354,12 +377,12 @@ def tile_custommodel_pb_t_kernel(tc, te, fe_n, loc_n, glob_n, logit_scale, logit
             take_second_rows(stream, 0)
             mend_first_rows(stream, 0)
         for step in range(len(rounds) + LAG):
-            to_quantise = [(s, step - 1) for s in order(step - 1)] if 1 <= step <= len(rounds) else []
+            to_quantise = [(part, step - 1) for part in joined(step - 1)] if 1 <= step <= len(rounds) else []
             to_exchange = [(s, step + 1) for s in order(step + 1)] if 1 <= step < len(rounds) - 1 else []
             for kind, i in VORDER:
                 if kind == "q":
                     for rows in to_quantise[i : i + 1]:
-                        quantise(rows[0], rows[1], grouped_of[rows])
+                        quantise(*rows)
                 elif kind == "t":
                     for rows in to_exchange[i : i + 1]:
                         take_second_rows(*rows)
@@ -382,12 +405,13 @@ def tile_custommodel_pb_t_kernel(tc, te, fe_n, loc_n, glob_n, logit_scale, logit
             if step == pool_step + 1:
                 sum_early()
 
-            if step >= LAG:
-                to_multiply.extend(rounds[step - LAG])
+            while multiplied < len(rounds) and multiplied <= step - (LAG if step < CATCH else LATE):
+                to_multiply.extend(rounds[multiplied])
+                multiplied += 1
             if step < len(rounds):
                 for stream in order(step):
                     vector_copies = (0,) if step >= len(rounds) - VTAIL and stream == order(step)[VT] else ()
-                    grouped_of[(stream, step)] = transpose_rows(stream, step, vector_copies)
+                    transpose_rows(stream, step, vector_copies)
                     if step == 0 and stream == FE:
                         transpose_te(False, nc.vector.tensor_copy)
                         transpose_te(True, nc.vector.tensor_copy)
@@ -405,7 +429,7 @@ def tile_custommodel_pb_t_kernel(tc, te, fe_n, loc_n, glob_n, logit_scale, logit
                     mend_first_rows(stream, 1)
             if step == 1:
                 nc.scalar.activation(out=gain[:], in_=scale_raw[:], func=ACT.Exp)
-            while to_multiply:
+            while to_multiply and not (DEFER <= step < len(rounds) - 1):
                 multiply_next()
         for done in finished:
             maximise(done)

@@ -37,7 +37,8 @@ FE, LOC, GLOB = 0, 1, 2
 PSUM_BANKS = 8
 PRODUCT_BANKS = 2
 PAIR = 2
-AHEAD = 8
+QFROM = 3
+AHEAD = 3
 ROUNDS = [PAIR] * 15 + [1, 1]
 GROUPS = [4] * 7 + [2, 1, 1]
 LAG = 2
@@ -101,7 +102,8 @@ def tile_custommodel_pb_t_kernel(tc, te, fe_n, loc_n, glob_n, logit_scale, logit
                 loaded[(stream, step)] = x
             m = first + (count or len(tiles))
             c, j = tiles[0] // CLIP, tiles[0] % CLIP
-            nc.sync.dma_start(
+            queue = nc.scalar if step >= QFROM and (step * 3 + order(step).index(stream)) % 2 == 1 else nc.sync
+            queue.dma_start(
                 out=loaded[(stream, step)][:, first:m, :], in_=streams[stream][:, c, j + first : j + m, :]
             )
 
@@ -150,8 +152,8 @@ def tile_custommodel_pb_t_kernel(tc, te, fe_n, loc_n, glob_n, logit_scale, logit
 
         identity = keep.tile([P, P], F32, name="identity")
         make_identity(nc, identity[:])
-        pooled_parts = keep.tile([P, 2, P], F32, name="pooled_parts")
-        nc.gpsimd.memset(pooled_parts[:], 0.0)
+        pooled = keep.tile([P, P], F32, name="pooled")
+        nc.gpsimd.memset(pooled[:], 0.0)
         blank = keep.tile([P, 1], F32, name="blank")
         nc.gpsimd.memset(blank[:], 0.0)
         one = keep.tile([P, 1], F32, name="one")
@@ -307,6 +309,8 @@ def tile_custommodel_pb_t_kernel(tc, te, fe_n, loc_n, glob_n, logit_scale, logit
 
         terms = keep.tile([P, 2, CLIPS_PER_PARTITION, CLIP], F32, name="terms")
         top = keep.tile([P, CLIPS_PER_PARTITION], F32, name="top")
+        sums = keep.tile([P, 2, CLIPS_PER_PARTITION], F32, name="sums")
+        inverse = keep.tile([P, CLIPS_PER_PARTITION], F32, name="inverse")
         shifted = keep.tile([P, CLIPS_PER_PARTITION, CLIP], F32, name="shifted")
 
         def shift_early():
@@ -332,9 +336,9 @@ def tile_custommodel_pb_t_kernel(tc, te, fe_n, loc_n, glob_n, logit_scale, logit
             nc.vector.tensor_tensor(
                 out=terms[:, 0, clips, :], in0=terms[:, 1, clips, :], in1=logits[:, clips, :], op=ALU.mult
             )
-            nc.vector.tensor_reduce(
-                out=pooled_parts[:, :, clips], in_=terms[:, :, clips, :], axis=AXIS.X, op=ALU.add
-            )
+            nc.vector.tensor_reduce(out=sums[:, :, clips], in_=terms[:, :, clips, :], axis=AXIS.X, op=ALU.add)
+            nc.vector.reciprocal(out=inverse[:, clips], in_=sums[:, 1, clips])
+            nc.vector.tensor_tensor(out=pooled[:, clips], in0=sums[:, 0, clips], in1=inverse[:, clips], op=ALU.mult)
 
         def pool_last():
             c = EARLY_CLIPS
@@ -347,17 +351,18 @@ def tile_custommodel_pb_t_kernel(tc, te, fe_n, loc_n, glob_n, logit_scale, logit
                 in_=shifted[:, c, :],
                 func=ACT.Exp,
                 scale=side_gain[:, 0:1],
-                accum_out=pooled_parts[:, 1, c : c + 1],
+                accum_out=sums[:, 1, c : c + 1],
             )
             weigh(slice(c, c + 1))
+            nc.vector.reciprocal(out=inverse[:, c : c + 1], in_=sums[:, 1, c : c + 1])
             nc.vector.scalar_tensor_tensor(
                 out=terms[:, 0, c, :],
                 in0=terms[:, 1, c, :],
-                scalar=1.0,
+                scalar=inverse[:, c : c + 1],
                 in1=logits[:, c, :],
                 op0=ALU.mult,
                 op1=ALU.mult,
-                accum_out=pooled_parts[:, 0, c : c + 1],
+                accum_out=pooled[:, c : c + 1],
             )
 
         grouped_of = {}
@@ -435,13 +440,8 @@ def tile_custommodel_pb_t_kernel(tc, te, fe_n, loc_n, glob_n, logit_scale, logit
             maximise(done)
         pool_last()
 
-        turned = banks.tile([P, 2, P], F32, name="turned", tag="bank")
-        for h in range(2):
-            nc.tensor.transpose(turned[:, h, :], pooled_parts[:, h, :], identity[:])
-        inverse = keep.tile([CLIPS_PER_PARTITION, P], F32, name="inverse")
-        nc.vector.reciprocal(out=inverse[:], in_=turned[0:CLIPS_PER_PARTITION, 1, :])
-        pooled = keep.tile([CLIPS_PER_PARTITION, P], F32, name="pooled")
-        nc.vector.tensor_tensor(
-            out=pooled[:], in0=turned[0:CLIPS_PER_PARTITION, 0, :], in1=inverse[:], op=ALU.mult
-        )
-        nc.sync.dma_start(out=out.rearrange("o (c p) -> (o c) p", p=P), in_=pooled[:])
+        turned = banks.tile([P, P], F32, name="turned", tag="bank")
+        nc.tensor.transpose(turned[:], pooled[:], identity[:])
+        rows = keep.tile([CLIPS_PER_PARTITION, P], F32, name="rows")
+        nc.vector.tensor_copy(out=rows[:], in_=turned[0:CLIPS_PER_PARTITION, :])
+        nc.sync.dma_start(out=out.rearrange("o (c p) -> (o c) p", p=P), in_=rows[:])

from contextlib import ExitStack

import concourse.mybir as mybir
from concourse.masks import make_identity

F32 = mybir.dt.float32
BF16 = mybir.dt.bfloat16
U32 = mybir.dt.uint32
U8 = mybir.dt.uint8
FP8X4 = mybir.dt.float8_e4m3fn_x4
ALU = mybir.AluOpType
ACT = mybir.ActivationFunctionType
AXIS = mybir.AxisListType

P = 128
FRAMES = 4096
FEATURES = 1024
QUERIES = 128
CLIP = 8
SIDE_WEIGHT = 0.05
MAIN_FACTORS = (16, 2)

FLOPS = 2 * 3 * QUERIES * FRAMES * FEATURES

TILES = FRAMES // P
CLIPS_PER_PARTITION = TILES // CLIP
K_PASS = 4 * P
PASSES = FEATURES // K_PASS
WORDS = FEATURES // 2
WORD_BLOCKS = WORDS // P
HALVES = WORD_BLOCKS // PASSES
MX_BLOCKS = P // 8
HALF_BLOCK = 16

FE, LOC, GLOB = 0, 1, 2

PSUM_BANKS = 8
PRODUCT_BANKS = 2
PAIR = 2
QFROM = 3
AHEAD = 3
ROUNDS = [PAIR] * 15 + [1, 1]
GROUPS = [4] * 7 + [2, 1, 1]
LAG = 2
TE_FORMS = [(True, 1), (False, 1), (False, 16), (False, 2)]
VORDER = [("q", 0), ("t", 0), ("q", 1), ("m", 0), ("t", 1), ("m", 1), ("t", 2), ("m", 2)]
OSTEP = 1
EXPAT = 2
FIRST = 1
JOIN = 2
LASTS = 1
CATCH = 100
LATE = 1
FREEBANKS = True
DEFER = 15
VTAIL = 0
VT = 1
EARLY_CLIPS = 3
TE_STEP = 1
TE_AFTER = 1


def order(step):
    return (LOC, GLOB, FE) if step >= OSTEP else (FE, LOC, GLOB)


def split(counts):
    runs = []
    first = 0
    for count in counts:
        runs.append(list(range(first, first + count)))
        first += count
    return runs


def tile_custommodel_pb_t_kernel(tc, te, fe_n, loc_n, glob_n, logit_scale, logit_bias, out):
    nc = tc.nc
    streams = {}
    for stream, hbm in ((FE, fe_n), (LOC, loc_n), (GLOB, glob_n)):
        streams[stream] = hbm.rearrange("(c p j) d -> p c j d", c=CLIPS_PER_PARTITION, j=CLIP)

    rounds = split(ROUNDS)
    groups = split(GROUPS)
    group_of = {t: group for group in groups for t in group}

    with ExitStack() as ctx:
        keep = ctx.enter_context(tc.tile_pool(name="keep", bufs=1))
        frames = ctx.enter_context(tc.tile_pool(name="frames", bufs=3 * AHEAD))
        ordered = ctx.enter_context(tc.tile_pool(name="ordered", bufs=6))
        stage = ctx.enter_context(tc.tile_pool(name="stage", bufs=3))
        packed = ctx.enter_context(tc.tile_pool(name="packed", bufs=4))
        banks = ctx.enter_context(tc.psum_pool(name="banks", bufs=PSUM_BANKS - PRODUCT_BANKS))
        products = ctx.enter_context(tc.psum_pool(name="products", bufs=PRODUCT_BANKS))
        ctx.enter_context(tc.manual_schedule())

        loaded = {}

        def load(stream, step, first=0, count=None):
            tiles = rounds[step]
            if first == 0:
                x = frames.tile([P, len(tiles), FEATURES], BF16, name="x")
                loaded[(stream, step)] = x
            m = first + (count or len(tiles))
            c, j = tiles[0] // CLIP, tiles[0] % CLIP
            queue = nc.scalar if step >= QFROM and (step * 3 + order(step).index(stream)) % 2 == 1 else nc.sync
            queue.dma_start(
                out=loaded[(stream, step)][:, first:m, :], in_=streams[stream][:, c, j + first : j + m, :]
            )

        def take_second(rows, second):
            nc.vector.tensor_copy(
                out=second.rearrange("p (k m v i) -> p k m v i", m=MX_BLOCKS // 2, v=HALVES, i=HALF_BLOCK),
                in_=rows.rearrange("p (k v m e i) -> p e k m v i", v=HALVES, m=MX_BLOCKS // 2, e=2, i=HALF_BLOCK)[:, 1],
            )

        def mend_first(rows):
            view = rows.rearrange("p (k v m e i) -> p v e k m i", v=HALVES, m=MX_BLOCKS // 2, e=2, i=HALF_BLOCK)
            nc.vector.tensor_copy(out=view[:, 0, 1], in_=view[:, 1, 0])

        def transpose_words(first, second, bank):
            words = first.bitcast(F32)
            for g in range(PASSES):
                for u in range(HALVES):
                    start = g * HALVES * P
                    if not second:
                        run = words[:, start + u : start + HALVES * P : HALVES]
                    elif u == 0:
                        run = words[:, start : start + P]
                    else:
                        run = second[0].bitcast(F32)[:, g * P : (g + 1) * P]
                    nc.tensor.transpose(bank[:, g * HALVES + u, :], run, identity[:])

        def regroup(copy, bank, grouped_rows):
            copy(
                out=grouped_rows.bitcast(F32).rearrange("p (g r u) -> p g r u", g=PASSES, u=HALVES),
                in_=bank[:].rearrange("p (g u) r -> p g r u", u=HALVES),
            )

        te_rows = keep.tile([P, FEATURES], BF16, name="te_rows")
        scale_raw = keep.tile([P, 1], BF16, name="scale_raw")
        bias_raw = keep.tile([P, 1], BF16, name="bias_raw")
        first_pieces = [(stream, n) for stream in order(0) for n in range(len(rounds[0]))]
        for i, (stream, n) in enumerate(first_pieces):
            if i == TE_AFTER:
                nc.sync.dma_start(out=te_rows[:], in_=te)
            load(stream, 0, n, 1)
        nc.scalar.dma_start(out=scale_raw[:], in_=logit_scale.partition_broadcast(P))
        nc.scalar.dma_start(out=bias_raw[:], in_=logit_bias.partition_broadcast(P))
        for step in range(1, AHEAD):
            for stream in order(step):
                load(stream, step)

        identity = keep.tile([P, P], F32, name="identity")
        make_identity(nc, identity[:])
        pooled = keep.tile([P, P], F32, name="pooled")
        nc.gpsimd.memset(pooled[:], 0.0)
        blank = keep.tile([P, 1], F32, name="blank")
        nc.gpsimd.memset(blank[:], 0.0)
        one = keep.tile([P, 1], F32, name="one")
        nc.scalar.activation(out=one[:], in_=blank[:], func=ACT.Exp)
        gain = keep.tile([P, 1], F32, name="gain")
        bias = keep.tile([P, 1], F32, name="bias")
        side_gain = keep.tile([P, 1], F32, name="side_gain")

        te_multiples = {}
        te_codes = {}
        te_scales = {}

        def transpose_te(exchanged, copy):
            second = []
            if exchanged:
                te_second = keep.tile([P, FEATURES // HALVES], BF16, name="te_second")
                take_second(te_rows[:], te_second[:])
                mend_first(te_rows[:])
                second = [te_second[:]]
            te_bank = products.tile([P, WORD_BLOCKS, P], F32, name="te_bank", tag="product")
            transpose_words(te_rows[:], second, te_bank)
            te_grouped = keep.tile([P, FEATURES], BF16, name="te_grouped_%d" % exchanged, align_bytes=64)
            regroup(copy, te_bank, te_grouped[:])
            te_multiples[(exchanged, 1)] = te_grouped

        def scale_te(exchanged, factor):
            rows = keep.tile([P, FEATURES], BF16, name="te_%d_times_%d" % (exchanged, factor), align_bytes=64)
            nc.gpsimd.tensor_scalar(
                out=rows[:],
                in0=te_multiples[(exchanged, 1)][:],
                scalar1=float(factor),
                scalar2=0.0,
                op0=ALU.mult,
                op1=ALU.add,
            )
            te_multiples[(exchanged, factor)] = rows

        def quantise_te(exchanged, factor):
            codes = keep.tile([P, PASSES * QUERIES], U32, name="te_codes_%d_%d" % (exchanged, factor), align_bytes=64)
            scales = keep.tile([P, PASSES * QUERIES], U8, name="te_scales_%d_%d" % (exchanged, factor), align_bytes=64)
            rows = te_multiples[(exchanged, factor)]
            nc.vector.quantize_mx(out=codes[:].bitcast(FP8X4), scales=scales[:], in_=rows[:])
            te_codes[(exchanged, factor)] = codes
            te_scales[(exchanged, factor)] = scales

        peaks = keep.tile([P, CLIPS_PER_PARTITION, CLIP], F32, name="peaks")
        flat_peaks = peaks[:].rearrange("p c j -> p (c j)")
        logits = keep.tile([P, CLIPS_PER_PARTITION, CLIP], F32, name="logits")

        def is_exchanged(stream, step):
            return stream != FE and FIRST <= step < len(rounds) - LASTS

        second_of = {}

        def pieces_of(step):
            count = len(rounds[step])
            piece = 1 if step == 0 else count
            return [slice(n, n + piece) for n in range(0, count, piece)]

        def flat(rows):
            return rows.rearrange("p t d -> p (t d)")

        def take_second_rows(stream, step):
            if not is_exchanged(stream, step):
                return
            second = ordered.tile([P, len(rounds[step]), FEATURES // HALVES], BF16, name="second")
            second_of[(stream, step)] = second
            for part in pieces_of(step):
                take_second(flat(loaded[(stream, step)][:, part, :]), flat(second[:, part, :]))

        def mend_first_rows(stream, step):
            if not is_exchanged(stream, step):
                return
            for part in pieces_of(step):
                mend_first(flat(loaded[(stream, step)][:, part, :]))

        def joined(step):
            names = order(step)
            return [names[:JOIN]] + [names[i : i + 1] for i in range(JOIN, len(names))]

        def transpose_rows(stream, step, vector_copies):
            count = len(rounds[step])
            part = [names for names in joined(step) if stream in names][0]
            if stream == part[0]:
                grouped = stage.tile(
                    [P, len(part) * count * FEATURES], BF16, name="grouped%d" % len(part), align_bytes=64
                )
                grouped_of[(part, step)] = grouped
            first = part.index(stream) * count
            for n in range(count):
                bank = banks.tile([P, WORD_BLOCKS, P], F32, name="bank")
                second = [second_of[(stream, step)][:, n, :]] if is_exchanged(stream, step) else []
                transpose_words(loaded[(stream, step)][:, n, :], second, bank)
                copy = nc.vector.tensor_copy if n in vector_copies else nc.scalar.copy
                cols = slice((first + n) * FEATURES, (first + n + 1) * FEATURES)
                regroup(copy, bank, grouped_of[(part, step)][:, cols])

        quantised = {}

        def quantise(part, step):
            count = len(rounds[step])
            width = len(part) * count * PASSES * P
            codes = packed.tile([P, width], U32, name="codes%d" % len(part), align_bytes=64)
            scales = packed.tile([P, width], U8, name="scales%d" % len(part), align_bytes=64)
            nc.vector.quantize_mx(
                out=codes[:].bitcast(FP8X4), scales=scales[:], in_=grouped_of[(part, step)][:]
            )
            for i, stream in enumerate(part):
                for n, t in enumerate(rounds[step]):
                    quantised[(stream, t)] = (codes, scales, i * count + n, is_exchanged(stream, step))

        current = {}

        def multiply(t):
            group = group_of[t]
            if t == group[0]:
                if len(group) == max(GROUPS) or not FREEBANKS:
                    product = products.tile([P, max(GROUPS), QUERIES], F32, name="product")
                else:
                    product = banks.tile([P, max(GROUPS), QUERIES], F32, name="last_product", tag="bank")
                current["product"] = product
            passes = [(stream, 1, g) for stream in (LOC, GLOB) for g in range(PASSES)]
            passes += [(FE, factor, g) for factor in MAIN_FACTORS for g in range(PASSES)]
            for i, (stream, factor, g) in enumerate(passes):
                codes, scales, n, exchanged = quantised[(stream, t)]
                cols = slice((n * PASSES + g) * P, (n * PASSES + g + 1) * P)
                te_cols = slice(g * QUERIES, (g + 1) * QUERIES)
                nc.tensor.matmul_mx(
                    out=current["product"][:, t - group[0], :],
                    lhsT=codes[:, cols].bitcast(FP8X4),
                    lhsT_scale=scales[:, cols],
                    rhs=te_codes[(exchanged, factor)][:, te_cols].bitcast(FP8X4),
                    rhs_scale=te_scales[(exchanged, factor)][:, te_cols],
                    start=(i == 0),
                    stop=(i == len(passes) - 1),
                )
            return (group, current["product"]) if t == group[-1] else None

        def maximise(done):
            group, product = done
            cols = flat_peaks[:, group[0] : group[-1] + 1]
            nc.vector.tensor_reduce(out=cols, in_=product[:, : len(group), :], axis=AXIS.X, op=ALU.max)

        def weigh(clips):
            nc.vector.tensor_scalar(
                out=logits[:, clips, :],
                in0=peaks[:, clips, :],
                scalar1=side_gain[:, 0:1],
                scalar2=bias[:, 0:1],
                op0=ALU.mult,
                op1=ALU.add,
            )

        terms = keep.tile([P, 2, CLIPS_PER_PARTITION, CLIP], F32, name="terms")
        top = keep.tile([P, CLIPS_PER_PARTITION], F32, name="top")
        sums = keep.tile([P, 2, CLIPS_PER_PARTITION], F32, name="sums")
        inverse = keep.tile([P, CLIPS_PER_PARTITION], F32, name="inverse")
        shifted = keep.tile([P, CLIPS_PER_PARTITION, CLIP], F32, name="shifted")

        def shift_early():
            clips = slice(0, EARLY_CLIPS)
            shape = [P, EARLY_CLIPS, CLIP]
            nc.vector.tensor_reduce(out=top[:, clips], in_=peaks[:, clips, :], axis=AXIS.X, op=ALU.max)
            nc.vector.tensor_tensor(
                out=shifted[:, clips, :],
                in0=peaks[:, clips, :],
                in1=top[:, clips].unsqueeze(2).to_broadcast(shape),
                op=ALU.subtract,
            )
            weigh(clips)

        def exponentiate_early():
            clips = slice(0, EARLY_CLIPS)
            nc.scalar.activation(
                out=terms[:, 1, clips, :], in_=shifted[:, clips, :], func=ACT.Exp, scale=side_gain[:, 0:1]
            )

        def sum_early():
            clips = slice(0, EARLY_CLIPS)
            nc.vector.tensor_tensor(
                out=terms[:, 0, clips, :], in0=terms[:, 1, clips, :], in1=logits[:, clips, :], op=ALU.mult
            )
            nc.vector.tensor_reduce(out=sums[:, :, clips], in_=terms[:, :, clips, :], axis=AXIS.X, op=ALU.add)
            nc.vector.reciprocal(out=inverse[:, clips], in_=sums[:, 1, clips])
            nc.vector.tensor_tensor(out=pooled[:, clips], in0=sums[:, 0, clips], in1=inverse[:, clips], op=ALU.mult)

        def pool_last():
            c = EARLY_CLIPS
            nc.vector.tensor_reduce(out=top[:, c : c + 1], in_=peaks[:, c, :], axis=AXIS.X, op=ALU.max)
            nc.vector.tensor_scalar(
                out=shifted[:, c, :], in0=peaks[:, c, :], scalar1=top[:, c : c + 1], scalar2=None, op0=ALU.subtract
            )
            nc.scalar.activation(
                out=terms[:, 1, c, :],
                in_=shifted[:, c, :],
                func=ACT.Exp,
                scale=side_gain[:, 0:1],
                accum_out=sums[:, 1, c : c + 1],
            )
            weigh(slice(c, c + 1))
            nc.vector.reciprocal(out=inverse[:, c : c + 1], in_=sums[:, 1, c : c + 1])
            nc.vector.scalar_tensor_tensor(
                out=terms[:, 0, c, :],
                in0=terms[:, 1, c, :],
                scalar=inverse[:, c : c + 1],
                in1=logits[:, c, :],
                op0=ALU.mult,
                op1=ALU.mult,
                accum_out=pooled[:, c : c + 1],
            )

        grouped_of = {}
        finished = []
        to_multiply = []
        multiplied = 0
        pool_step = len(rounds) + LAG

        def multiply_next():
            t = to_multiply[0]
            to_multiply.remove(t)
            done = multiply(t)
            if done:
                finished.append(done)

        for stream in order(0):
            take_second_rows(stream, 0)
            mend_first_rows(stream, 0)
        for step in range(len(rounds) + LAG):
            to_quantise = [(part, step - 1) for part in joined(step - 1)] if 1 <= step <= len(rounds) else []
            to_exchange = [(s, step + 1) for s in order(step + 1)] if 1 <= step < len(rounds) - 1 else []
            for kind, i in VORDER:
                if kind == "q":
                    for rows in to_quantise[i : i + 1]:
                        quantise(*rows)
                elif kind == "t":
                    for rows in to_exchange[i : i + 1]:
                        take_second_rows(*rows)
                else:
                    for rows in to_exchange[i : i + 1]:
                        mend_first_rows(*rows)
            if step == TE_STEP:
                for exchanged, factor in TE_FORMS:
                    quantise_te(exchanged, factor)
            if step == 3:
                nc.vector.tensor_copy(out=bias[:], in_=bias_raw[:])
                nc.vector.tensor_scalar_mul(out=side_gain[:], in0=gain[:], scalar1=SIDE_WEIGHT)
            for done in finished:
                maximise(done)
                if done[0][-1] == EARLY_CLIPS * CLIP - 1:
                    pool_step = step
            finished.clear()
            if step == pool_step:
                shift_early()
            if step == pool_step + 1:
                sum_early()

            while multiplied < len(rounds) and multiplied <= step - (LAG if step < CATCH else LATE):
                to_multiply.extend(rounds[multiplied])
                multiplied += 1
            if step < len(rounds):
                for stream in order(step):
                    vector_copies = (0,) if step >= len(rounds) - VTAIL and stream == order(step)[VT] else ()
                    transpose_rows(stream, step, vector_copies)
                    if step == 0 and stream == FE:
                        transpose_te(False, nc.vector.tensor_copy)
                        transpose_te(True, nc.vector.tensor_copy)
                    if step == pool_step and stream == order(step)[EXPAT]:
                        exponentiate_early()
                if step + AHEAD < len(rounds):
                    for stream in order(step + AHEAD):
                        load(stream, step + AHEAD)
            if step == 0:
                for exchanged, factor in TE_FORMS:
                    if factor != 1:
                        scale_te(exchanged, factor)
                for stream in order(1):
                    take_second_rows(stream, 1)
                    mend_first_rows(stream, 1)
            if step == 1:
                nc.scalar.activation(out=gain[:], in_=scale_raw[:], func=ACT.Exp)
            while to_multiply and not (DEFER <= step < len(rounds) - 1):
                multiply_next()
        for done in finished:
            maximise(done)
        pool_last()

        turned = banks.tile([P, P], F32, name="turned", tag="bank")
        nc.tensor.transpose(turned[:], pooled[:], identity[:])
        rows = keep.tile([CLIPS_PER_PARTITION, P], F32, name="rows")
        nc.vector.tensor_copy(out=rows[:], in_=turned[0:CLIPS_PER_PARTITION, :])
        nc.sync.dma_start(out=out.rearrange("o (c p) -> (o c) p", p=P), in_=rows[:])
